import numpy as np
import ml_dtypes


def mxq(x, axis, fmt="e4m3"):
    dtype, down = {"e4m3": (ml_dtypes.float8_e4m3fn, 7), "e5m2": (ml_dtypes.float8_e5m2, 14)}[fmt]
    v = np.moveaxis(np.asarray(x, np.float32).astype(ml_dtypes.bfloat16).astype(np.float64), axis, -1)
    blocks = v.reshape(v.shape[:-1] + (-1, 32))
    amax = np.abs(blocks).max(-1, keepdims=True)
    byte = np.maximum(np.where(amax > 0, np.frexp(amax)[1] - 1 + 127, 0) - down, 1)
    scale = np.exp2(byte - 127.0)
    codes = (blocks / scale).astype(np.float32).astype(dtype).astype(np.float64)
    return np.moveaxis((codes * scale).reshape(v.shape), -1, axis)


WIDE = False


def mx_kscale(k):
    if not WIDE:
        return np.ones(k)
    levels = np.array([10, -10, 5, -5, 0])
    if k % 512:
        return np.exp2(np.random.permutation(np.resize(levels, k // 32))).repeat(32)
    a = np.empty((k // 512, 16))
    for p in range(k // 512):
        a[p, :8] = np.random.permutation(np.resize(levels, 8))
        for g in range(8):
            far = levels[np.abs(levels - a[p, g]) >= 10]
            a[p, g + 8] = far[np.random.randint(len(far))]
    return np.exp2(a.ravel()).repeat(32)


BF16 = ml_dtypes.bfloat16


def bf(x):
    return np.asarray(x, np.float32).astype(BF16)


def f64(x):
    return np.asarray(x).astype(np.float64)


B, N, DI, D, H, DO = 8, 1024, 512, 256, 4, 1024
DH = D // H
SIG = 0.5


def time_concat(space):
    t = np.sqrt(1.0 + np.sum(space * space, axis=-1, keepdims=True))
    return np.concatenate([t, space], axis=-1)


def split_lift(space):
    return time_concat(space.reshape(B, N, H, DH).transpose(0, 2, 1, 3))


def setup_inputs():
    s = mx_kscale(DI)
    return {"x_space": bf(np.random.standard_normal((B, N, DI)) * s),
            "Wq": bf(np.random.standard_normal((D, DI)) * SIG / np.sqrt(DI) / s),
            "bq": bf(np.random.standard_normal(D) * 0.1),
            "Wk": bf(np.random.standard_normal((D, DI)) * SIG / np.sqrt(DI) / s),
            "bk": bf(np.random.standard_normal(D) * 0.1)}


def reference(x_space, Wq, bq, Wk, bk):
    xq = mxq(f64(x_space), 2, "e4m3")
    q = (xq @ mxq(f64(Wq), 1, "e4m3").T) + f64(bq)
    k = (xq @ mxq(f64(Wk), 1, "e4m3").T) + f64(bk)
    return split_lift(q), split_lift(k)

@@ -1,0 +1,231 @@
+from contextlib import ExitStack
+
+import concourse.mybir as mybir
+from concourse.masks import make_identity
+
+F32 = mybir.dt.float32
+BF16 = mybir.dt.bfloat16
+U32 = mybir.dt.uint32
+U8 = mybir.dt.uint8
+FP8X4 = mybir.dt.float8_e4m3fn_x4
+ADD = mybir.AluOpType.add
+SQUARE = mybir.ActivationFunctionType.Square
+SQRT = mybir.ActivationFunctionType.Sqrt
+
+P = 128
+BATCHES = 8
+TOKENS = 1024
+K = 512
+WORDS = K // 2
+FEATURES = 512
+HEAD = 64
+ROW = HEAD + 1
+TILES = TOKENS // P
+HALF = TILES // 2
+PIECE_HEADS = P // HEAD
+PIECE_ROWS = PIECE_HEADS * TILES
+PIECES_PER_BATCH = FEATURES // P
+PIECES = BATCHES * PIECES_PER_BATCH
+HALF_BATCHES = 2 * BATCHES
+ROUND_PIECES = PIECES // HALF_BATCHES
+
+LAG_QUANTISE = 1
+LAG_PROJECT = 3
+LAG_SQUARE = LAG_PROJECT + 1
+LAG_REDUCE = LAG_SQUARE + 1
+LAG_ROOT = LAG_REDUCE + 1
+
+SECOND_HALVING_EVERY = 2
+
+FLOPS = 2 * BATCHES * TOKENS * K * FEATURES
+
+
+def turn_two_tiles(nc, banks, identity, raw_words, grouped_words):
+    bank = banks.tile([P, 4 * P], F32)
+    for i in range(2):
+        for u in range(2):
+            nc.tensor.transpose(
+                bank[:, (2 * i + u) * P : (2 * i + u + 1) * P],
+                raw_words[:, i * WORDS + u : (i + 1) * WORDS : 2],
+                identity,
+            )
+    nc.scalar.copy(
+        out=grouped_words.rearrange("p (i r u) -> p i r u", i=2, u=2),
+        in_=bank[:].rearrange("p (i u r) -> p i r u", i=2, u=2),
+    )
+
+
+def tile_lorentzmultiheadattention_pa_t_kernel(tc, x_space, Wq, bq, Wk, bk, out_0, out_1):
+    nc = tc.nc
+    with ExitStack() as stack:
+        stack.enter_context(tc.manual_schedule())
+        const = stack.enter_context(tc.tile_pool(name="const", bufs=1))
+        x_pool = stack.enter_context(tc.tile_pool(name="x", bufs=2 * BATCHES))
+        mx_pool = stack.enter_context(tc.tile_pool(name="mx", bufs=4))
+        out_pool = stack.enter_context(tc.tile_pool(name="lifted", bufs=12))
+        sum_pool = stack.enter_context(tc.tile_pool(name="sums", bufs=4))
+        turn_banks = stack.enter_context(tc.psum_pool(name="turned", bufs=4))
+        product_banks = stack.enter_context(tc.psum_pool(name="products", bufs=4))
+
+        bias_row = const.tile([1, FEATURES], BF16)
+        nc.sync.dma_start(out=bias_row[:, 0 : FEATURES // 2], in_=bq.unsqueeze(0))
+        nc.sync.dma_start(out=bias_row[:, FEATURES // 2 : FEATURES], in_=bk.unsqueeze(0))
+        w_raw = const.tile([P, 4 * K], BF16)
+        nc.sync.dma_start(
+            out=w_raw[:, 0 : 2 * K].rearrange("p (c k) -> p c k", c=2), in_=Wq.rearrange("(c p) k -> p c k", p=P)
+        )
+        nc.sync.dma_start(
+            out=w_raw[:, 2 * K : 4 * K].rearrange("p (c k) -> p c k", c=2), in_=Wk.rearrange("(c p) k -> p c k", p=P)
+        )
+        x_words = []
+        for b in range(BATCHES):
+            x_by_tile = x_space[b].rearrange("(p t) k -> p t k", t=TILES)
+            for half in range(2):
+                x_raw = x_pool.tile([P, HALF, K], BF16)
+                nc.sync.dma_start(out=x_raw[:], in_=x_by_tile[:, half * HALF : (half + 1) * HALF, :])
+                x_words.append(x_raw[:].rearrange("p t k -> p (t k)").bitcast(F32))
+
+        identity = const.tile([P, P], F32)
+        make_identity(nc, identity[:])
+        one = const.tile([P, 1], F32)
+        nc.vector.memset(one[:], 1.0)
+        warm = const.tile([P, 1], F32)
+        nc.scalar.activation(out=warm[:], in_=one[:], func=SQRT)
+
+        bias_rows = const.tile([P, FEATURES], BF16)
+        nc.vector.memset(bias_rows[:], 0.0)
+        nc.vector.tensor_copy(out=bias_rows[0:1, :], in_=bias_row[:])
+        ones = const.tile([P, P], BF16)
+        nc.vector.memset(ones[:], 1.0)
+        bias_bank = product_banks.tile([P, FEATURES], F32, tag="product")
+        nc.tensor.matmul(out=bias_bank[:], lhsT=ones[:], rhs=bias_rows[:], start=True, stop=True)
+        bias = const.tile([P, FEATURES], F32)
+        nc.vector.tensor_copy(out=bias[:], in_=bias_bank[:])
+
+        w_grouped = const.tile([P, 4 * FEATURES], BF16, align_bytes=64)
+        w_codes = const.tile([P, FEATURES], U32, align_bytes=64)
+        w_scales = const.tile([P, FEATURES], U8, align_bytes=64)
+        for j in range(2):
+            turn_two_tiles(
+                nc,
+                turn_banks,
+                identity[:],
+                w_raw[:].bitcast(F32)[:, 2 * j * WORDS : 2 * (j + 1) * WORDS],
+                w_grouped[:].bitcast(F32)[:, 4 * j * P : 4 * (j + 1) * P],
+            )
+        nc.vector.quantize_mx(out=w_codes[:].bitcast(FP8X4), scales=w_scales[:], in_=w_grouped[:])
+
+        grouped = {}
+        codes = {}
+        scales = {}
+        lifted = {}
+        partial_sums = {}
+        norms = {}
+
+        def turn(half_batch):
+            x_grouped = mx_pool.tile([P, 4 * HALF * P], BF16, align_bytes=64)
+            grouped[half_batch] = x_grouped
+            for j in range(HALF // 2):
+                turn_two_tiles(
+                    nc,
+                    turn_banks,
+                    identity[:],
+                    x_words[half_batch][:, 2 * j * WORDS : 2 * (j + 1) * WORDS],
+                    x_grouped[:].bitcast(F32)[:, 4 * j * P : 4 * (j + 1) * P],
+                )
+
+        def quantise(half_batch):
+            x_codes = mx_pool.tile([P, HALF * P], U32, align_bytes=64)
+            x_scales = mx_pool.tile([P, HALF * P], U8, align_bytes=64)
+            nc.vector.quantize_mx(out=x_codes[:].bitcast(FP8X4), scales=x_scales[:], in_=grouped[half_batch][:])
+            codes[half_batch] = x_codes
+            scales[half_batch] = x_scales
+
+        def project(piece):
+            b, c = divmod(piece, PIECES_PER_BATCH)
+            features = slice(c * P, (c + 1) * P)
+            rows = out_pool.tile([P, PIECE_ROWS, ROW], F32)
+            lifted[piece] = rows
+            u_by_tile = rows[:, :, 1:ROW].rearrange("p (h t) d -> p t h d", h=PIECE_HEADS)
+            bias_by_tile = (
+                bias[:, features]
+                .rearrange("p (h d) -> p h d", h=PIECE_HEADS)
+                .unsqueeze(1)
+                .to_broadcast([P, HALF, PIECE_HEADS, HEAD])
+            )
+            for half in range(2):
+                half_batch = 2 * b + half
+                product = product_banks.tile([P, HALF * P], F32)
+                for i in range(HALF):
+                    tokens = slice(i * P, (i + 1) * P)
+                    nc.tensor.matmul_mx(
+                        out=product[:, tokens],
+                        lhsT=codes[half_batch][:, tokens].bitcast(FP8X4),
+                        lhsT_scale=scales[half_batch][:, tokens],
+                        rhs=w_codes[:, features].bitcast(FP8X4),
+                        rhs_scale=w_scales[:, features],
+                        start=True,
+                        stop=True,
+                    )
+                nc.vector.tensor_tensor(
+                    out=u_by_tile[:, half * HALF : (half + 1) * HALF],
+                    in0=product[:].rearrange("p (t h d) -> p t h d", t=HALF, h=PIECE_HEADS),
+                    in1=bias_by_tile,
+                    op=ADD,
+                )
+
+        def square(piece):
+            squares = sum_pool.tile([P, PIECE_ROWS, HEAD], F32)
+            nc.scalar.activation(out=squares[:], in_=lifted[piece][:, :, 1:ROW], func=SQUARE)
+            partial_sums[piece] = squares
+            if piece >= PIECES - ROUND_PIECES:
+                return
+            half_sums = sum_pool.tile([P, PIECE_ROWS, HEAD // 2], F32)
+            nc.gpsimd.tensor_tensor(
+                out=half_sums[:], in0=squares[:, :, 0 : HEAD // 2], in1=squares[:, :, HEAD // 2 : HEAD], op=ADD
+            )
+            partial_sums[piece] = half_sums
+            if piece % SECOND_HALVING_EVERY == 0:
+                quarter_sums = sum_pool.tile([P, PIECE_ROWS, HEAD // 4], F32)
+                nc.gpsimd.tensor_tensor(
+                    out=quarter_sums[:],
+                    in0=half_sums[:, :, 0 : HEAD // 4],
+                    in1=half_sums[:, :, HEAD // 4 : HEAD // 2],
+                    op=ADD,
+                )
+                partial_sums[piece] = quarter_sums
+
+        def reduce_rows(piece):
+            norm = sum_pool.tile([P, PIECE_ROWS], F32)
+            nc.vector.tensor_reduce(out=norm[:], in_=partial_sums[piece][:], axis=mybir.AxisListType.X, op=ADD)
+            norms[piece] = norm
+
+        def root_and_store(piece):
+            b, c = divmod(piece, PIECES_PER_BATCH)
+            rows = lifted[piece]
+            nc.scalar.activation(out=rows[:, :, 0], in_=norms[piece][:], func=SQRT, bias=one[:])
+            target = (out_0, out_1)[c // 2]
+            first_head = PIECE_HEADS * (c % 2)
+            nc.sync.dma_start(
+                out=target[b, first_head : first_head + PIECE_HEADS].rearrange("h (p t) d -> p h (t d)", t=TILES),
+                in_=rows[:].rearrange("p (h t) d -> p h (t d)", h=PIECE_HEADS),
+            )
+
+        def pieces_of(r):
+            if 0 <= r < HALF_BATCHES:
+                return range(ROUND_PIECES * r, ROUND_PIECES * (r + 1))
+            return range(0)
+
+        for r in range(HALF_BATCHES + LAG_ROOT):
+            for piece in pieces_of(r - LAG_PROJECT):
+                project(piece)
+            if 0 <= r - LAG_QUANTISE < HALF_BATCHES:
+                quantise(r - LAG_QUANTISE)
+            for piece in pieces_of(r - LAG_SQUARE):
+                square(piece)
+            if r < HALF_BATCHES:
+                turn(r)
+            for piece in pieces_of(r - LAG_REDUCE):
+                reduce_rows(piece)
+            for piece in pieces_of(r - LAG_ROOT):
+                root_and_store(piece)

@@ -22,37 +22,25 @@ HEAD = 64
 ROW = HEAD + 1
 TILES = TOKENS // P
 HALF = TILES // 2
+UNIT = 2
+UNITS_PER_BATCH = TILES // UNIT
+UNITS = BATCHES * UNITS_PER_BATCH
 PIECE_HEADS = P // HEAD
 PIECE_ROWS = PIECE_HEADS * TILES
 PIECES_PER_BATCH = FEATURES // P
 PIECES = BATCHES * PIECES_PER_BATCH
-HALF_BATCHES = 2 * BATCHES
-ROUND_PIECES = PIECES // HALF_BATCHES
 
-LAG_QUANTISE = 1
-LAG_PROJECT = 3
-LAG_SQUARE = LAG_PROJECT + 1
-LAG_REDUCE = LAG_SQUARE + 1
-LAG_ROOT = LAG_REDUCE + 1
+LAG_REDUCE = 2
+LAG_ROOT = 3
+QUANT = 2
+PAIR = 2
 
-SECOND_HALVING_EVERY = 2
+
+def METHOD(piece):
+    return "DEE"[piece % 3]
+
 
 FLOPS = 2 * BATCHES * TOKENS * K * FEATURES
-
-
-def turn_two_tiles(nc, banks, identity, raw_words, grouped_words):
-    bank = banks.tile([P, 4 * P], F32)
-    for i in range(2):
-        for u in range(2):
-            nc.tensor.transpose(
-                bank[:, (2 * i + u) * P : (2 * i + u + 1) * P],
-                raw_words[:, i * WORDS + u : (i + 1) * WORDS : 2],
-                identity,
-            )
-    nc.scalar.copy(
-        out=grouped_words.rearrange("p (i r u) -> p i r u", i=2, u=2),
-        in_=bank[:].rearrange("p (i u r) -> p i r u", i=2, u=2),
-    )
 
 
 def tile_lorentzmultiheadattention_pa_t_kernel(tc, x_space, Wq, bq, Wk, bk, out_0, out_1):
@@ -60,9 +48,9 @@ def tile_lorentzmultiheadattention_pa_t_kernel(tc, x_space, Wq, bq, Wk, bk, out_
     with ExitStack() as stack:
         stack.enter_context(tc.manual_schedule())
         const = stack.enter_context(tc.tile_pool(name="const", bufs=1))
-        x_pool = stack.enter_context(tc.tile_pool(name="x", bufs=2 * BATCHES))
+        x_pool = stack.enter_context(tc.tile_pool(name="x", bufs=1))
         mx_pool = stack.enter_context(tc.tile_pool(name="mx", bufs=4))
-        out_pool = stack.enter_context(tc.tile_pool(name="lifted", bufs=12))
+        out_pool = stack.enter_context(tc.tile_pool(name="lifted", bufs=10))
         sum_pool = stack.enter_context(tc.tile_pool(name="sums", bufs=4))
         turn_banks = stack.enter_context(tc.psum_pool(name="turned", bufs=4))
         product_banks = stack.enter_context(tc.psum_pool(name="products", bufs=4))
@@ -71,19 +59,32 @@ def tile_lorentzmultiheadattention_pa_t_kernel(tc, x_space, Wq, bq, Wk, bk, out_
         nc.sync.dma_start(out=bias_row[:, 0 : FEATURES // 2], in_=bq.unsqueeze(0))
         nc.sync.dma_start(out=bias_row[:, FEATURES // 2 : FEATURES], in_=bk.unsqueeze(0))
         w_raw = const.tile([P, 4 * K], BF16)
-        nc.sync.dma_start(
-            out=w_raw[:, 0 : 2 * K].rearrange("p (c k) -> p c k", c=2), in_=Wq.rearrange("(c p) k -> p c k", p=P)
-        )
-        nc.sync.dma_start(
-            out=w_raw[:, 2 * K : 4 * K].rearrange("p (c k) -> p c k", c=2), in_=Wk.rearrange("(c p) k -> p c k", p=P)
-        )
-        x_words = []
-        for b in range(BATCHES):
-            x_by_tile = x_space[b].rearrange("(p t) k -> p t k", t=TILES)
-            for half in range(2):
-                x_raw = x_pool.tile([P, HALF, K], BF16)
-                nc.sync.dma_start(out=x_raw[:], in_=x_by_tile[:, half * HALF : (half + 1) * HALF, :])
-                x_words.append(x_raw[:].rearrange("p t k -> p (t k)").bitcast(F32))
+        x_words = {}
+
+        def load_w(half, W):
+            nc.sync.dma_start(
+                out=w_raw[:, half * 2 * K : (half + 1) * 2 * K].rearrange("p (c k) -> p c k", c=2),
+                in_=W.rearrange("(c p) k -> p c k", p=P),
+            )
+
+        def load_x(first_unit, count):
+            b, u = divmod(first_unit, UNITS_PER_BATCH)
+            x_raw = x_pool.tile([P, count * UNIT, K], BF16, name="x%d" % first_unit)
+            nc.sync.dma_start(
+                out=x_raw[:],
+                in_=x_space[b].rearrange("(p t) k -> p t k", t=TILES)[:, u * UNIT : (u + count) * UNIT, :],
+            )
+            words = x_raw[:].rearrange("p t k -> p (t k)").bitcast(F32)
+            for i in range(count):
+                x_words[first_unit + i] = words[:, i * UNIT * WORDS : (i + 1) * UNIT * WORDS]
+
+        load_w(0, Wq)
+        load_x(0, 1)
+        load_w(1, Wk)
+        for u in range(1, UNITS_PER_BATCH):
+            load_x(u, 1)
+        for u in range(UNITS_PER_BATCH, UNITS, 2):
+            load_x(u, 2)
 
         identity = const.tile([P, P], F32)
         make_identity(nc, identity[:])
@@ -102,90 +103,156 @@ def tile_lorentzmultiheadattention_pa_t_kernel(tc, x_space, Wq, bq, Wk, bk, out_
         bias = const.tile([P, FEATURES], F32)
         nc.vector.tensor_copy(out=bias[:], in_=bias_bank[:])
 
+        def turn_two_tiles(raw_words, grouped_words, copy):
+            bank = turn_banks.tile([P, 4 * P], F32)
+            for i in range(2):
+                for u in range(2):
+                    nc.tensor.transpose(
+                        bank[:, (2 * i + u) * P : (2 * i + u + 1) * P],
+                        raw_words[:, i * WORDS + u : (i + 1) * WORDS : 2],
+                        identity[:],
+                    )
+            copy(
+                out=grouped_words.rearrange("p (i r u) -> p i r u", i=2, u=2),
+                in_=bank[:].rearrange("p (i u r) -> p i r u", i=2, u=2),
+            )
+
         w_grouped = const.tile([P, 4 * FEATURES], BF16, align_bytes=64)
         w_codes = const.tile([P, FEATURES], U32, align_bytes=64)
         w_scales = const.tile([P, FEATURES], U8, align_bytes=64)
-        for j in range(2):
+        H = FEATURES // 2
+
+        def turn_w(j):
             turn_two_tiles(
-                nc,
-                turn_banks,
-                identity[:],
                 w_raw[:].bitcast(F32)[:, 2 * j * WORDS : 2 * (j + 1) * WORDS],
                 w_grouped[:].bitcast(F32)[:, 4 * j * P : 4 * (j + 1) * P],
+                nc.vector.tensor_copy,
             )
-        nc.vector.quantize_mx(out=w_codes[:].bitcast(FP8X4), scales=w_scales[:], in_=w_grouped[:])
+
+        def quantise_w(j):
+            nc.vector.quantize_mx(
+                out=w_codes[:, j * H : (j + 1) * H].bitcast(FP8X4),
+                scales=w_scales[:, j * H : (j + 1) * H],
+                in_=w_grouped[:, 4 * j * H : 4 * (j + 1) * H],
+            )
 
         grouped = {}
+        whole = {}
         codes = {}
         scales = {}
         lifted = {}
+        squares_of = {}
+        stats_of = {}
         partial_sums = {}
         norms = {}
 
-        def turn(half_batch):
-            x_grouped = mx_pool.tile([P, 4 * HALF * P], BF16, align_bytes=64)
-            grouped[half_batch] = x_grouped
-            for j in range(HALF // 2):
-                turn_two_tiles(
-                    nc,
-                    turn_banks,
-                    identity[:],
-                    x_words[half_batch][:, 2 * j * WORDS : 2 * (j + 1) * WORDS],
-                    x_grouped[:].bitcast(F32)[:, 4 * j * P : 4 * (j + 1) * P],
-                )
+        def turn(unit, q=QUANT):
+            if unit % q == 0:
+                x_grouped = mx_pool.tile([P, 4 * UNIT * P * q], BF16, align_bytes=64)
+            for i in range(q):
+                if unit % q == 0:
+                    grouped[unit + i] = x_grouped[:, i * 4 * UNIT * P : (i + 1) * 4 * UNIT * P]
+                    whole[unit + i] = x_grouped
+            turn_two_tiles(x_words[unit], grouped[unit].bitcast(F32), nc.scalar.copy)
 
-        def quantise(half_batch):
-            x_codes = mx_pool.tile([P, HALF * P], U32, align_bytes=64)
-            x_scales = mx_pool.tile([P, HALF * P], U8, align_bytes=64)
-            nc.vector.quantize_mx(out=x_codes[:].bitcast(FP8X4), scales=x_scales[:], in_=grouped[half_batch][:])
-            codes[half_batch] = x_codes
-            scales[half_batch] = x_scales
+        def quantise(unit, q=QUANT):
+            b, u = divmod(unit, UNITS_PER_BATCH)
+            if u == 0:
+                x_codes = mx_pool.tile([P, TILES * P], U32, align_bytes=64)
+                x_scales = mx_pool.tile([P, TILES * P], U8, align_bytes=64)
+                codes[b] = x_codes
+                scales[b] = x_scales
+            cols = slice(u * UNIT * P, (u + q) * UNIT * P)
+            nc.vector.quantize_mx(
+                out=codes[b][:, cols].bitcast(FP8X4), scales=scales[b][:, cols], in_=whole[unit][:]
+            )
 
-        def project(piece):
+        def project(piece, half):
             b, c = divmod(piece, PIECES_PER_BATCH)
             features = slice(c * P, (c + 1) * P)
-            rows = out_pool.tile([P, PIECE_ROWS, ROW], F32)
-            lifted[piece] = rows
-            u_by_tile = rows[:, :, 1:ROW].rearrange("p (h t) d -> p t h d", h=PIECE_HEADS)
-            bias_by_tile = (
-                bias[:, features]
+            if half == 0:
+                rows = out_pool.tile([P, PIECE_ROWS, ROW], F32)
+                lifted[piece] = rows
+            product = product_banks.tile([P, HALF * P], F32)
+            for i in range(HALF):
+                tokens = slice((half * HALF + i) * P, (half * HALF + i + 1) * P)
+                nc.tensor.matmul_mx(
+                    out=product[:, i * P : (i + 1) * P],
+                    lhsT=codes[b][:, tokens].bitcast(FP8X4),
+                    lhsT_scale=scales[b][:, tokens],
+                    rhs=w_codes[:, features].bitcast(FP8X4),
+                    rhs_scale=w_scales[:, features],
+                    start=True,
+                    stop=True,
+                )
+            u_rows = lifted[piece][:, :, 1:ROW].rearrange("p (h t) d -> p h t d", h=PIECE_HEADS)
+            nc.vector.tensor_tensor(
+                out=u_rows[:, :, half * HALF : (half + 1) * HALF],
+                in0=product[:].rearrange("p (t h d) -> p h t d", t=HALF, h=PIECE_HEADS),
+                in1=bias[:, features]
                 .rearrange("p (h d) -> p h d", h=PIECE_HEADS)
-                .unsqueeze(1)
-                .to_broadcast([P, HALF, PIECE_HEADS, HEAD])
+                .unsqueeze(2)
+                .to_broadcast([P, PIECE_HEADS, HALF, HEAD]),
+                op=ADD,
             )
-            for half in range(2):
-                half_batch = 2 * b + half
-                product = product_banks.tile([P, HALF * P], F32)
-                for i in range(HALF):
-                    tokens = slice(i * P, (i + 1) * P)
-                    nc.tensor.matmul_mx(
-                        out=product[:, tokens],
-                        lhsT=codes[half_batch][:, tokens].bitcast(FP8X4),
-                        lhsT_scale=scales[half_batch][:, tokens],
-                        rhs=w_codes[:, features].bitcast(FP8X4),
-                        rhs_scale=w_scales[:, features],
-                        start=True,
-                        stop=True,
+
+        def square(piece, part, parts):
+            if part == 0:
+                squares = sum_pool.tile([P, PIECE_HEADS, TILES, HEAD], F32)
+                squares_of[piece] = squares
+            ts = slice(part * TILES // parts, (part + 1) * TILES // parts)
+            nc.scalar.activation(
+                out=squares_of[piece][:, :, ts],
+                in_=lifted[piece][:, :, 1:ROW].rearrange("p (h t) d -> p h t d", h=PIECE_HEADS)[:, :, ts],
+                func=SQUARE,
+            )
+
+        def accumulate(piece, part, parts):
+            if part == 0:
+                norm = sum_pool.tile([P, PIECE_HEADS, TILES], F32, name="norm")
+                norms[piece] = norm
+                junk = sum_pool.tile([P, PIECE_HEADS, TILES, HEAD], F32, name="squares")
+                squares_of[piece] = junk
+            rows = lifted[piece][:, :, 1:ROW].rearrange("p (h t) d -> p h t d", h=PIECE_HEADS)
+            for h in range(PIECE_HEADS):
+                for t in range(part * TILES // parts, (part + 1) * TILES // parts):
+                    nc.scalar.activation(
+                        out=squares_of[piece][:, h, t],
+                        in_=rows[:, h, t],
+                        func=SQUARE,
+                        accum_out=norms[piece][:, h, t : t + 1],
                     )
-                nc.vector.tensor_tensor(
-                    out=u_by_tile[:, half * HALF : (half + 1) * HALF],
-                    in0=product[:].rearrange("p (t h d) -> p t h d", t=HALF, h=PIECE_HEADS),
-                    in1=bias_by_tile,
-                    op=ADD,
+
+        def statistics(piece, part, parts):
+            if part == 0:
+                stats = sum_pool.tile([P, TILES, 2, 3], F32)
+                stats_of[piece] = stats
+            rows = lifted[piece][:, :, 1:ROW].rearrange("p (h t) d -> p h t d", h=PIECE_HEADS)
+            for t in range(part * TILES // parts, (part + 1) * TILES // parts):
+                nc.vector.bn_stats(
+                    out=stats_of[piece][:, t].rearrange("p h s -> p (h s)"),
+                    in_=rows[:, :, t].rearrange("p h d -> p d h"),
                 )
 
-        def square(piece):
-            squares = sum_pool.tile([P, PIECE_ROWS, HEAD], F32)
-            nc.scalar.activation(out=squares[:], in_=lifted[piece][:, :, 1:ROW], func=SQUARE)
+        def combine(piece):
+            stats = stats_of[piece][:].rearrange("p t h s -> p h t s")
+            mean_part = sum_pool.tile([P, PIECE_HEADS, TILES], F32)
+            nc.scalar.activation(out=mean_part[:], in_=stats[:, :, :, 1], func=SQUARE, scale=8.0)
+            norm = sum_pool.tile([P, PIECE_HEADS, TILES], F32, name="norm")
+            nc.gpsimd.tensor_tensor(out=norm[:], in0=mean_part[:], in1=stats[:, :, :, 2], op=ADD)
+            norms[piece] = norm
+
+        def halve(piece):
+            squares = squares_of[piece][:].rearrange("p h t d -> p (h t) d")
             partial_sums[piece] = squares
-            if piece >= PIECES - ROUND_PIECES:
-                return
-            half_sums = sum_pool.tile([P, PIECE_ROWS, HEAD // 2], F32)
-            nc.gpsimd.tensor_tensor(
-                out=half_sums[:], in0=squares[:, :, 0 : HEAD // 2], in1=squares[:, :, HEAD // 2 : HEAD], op=ADD
-            )
-            partial_sums[piece] = half_sums
-            if piece % SECOND_HALVING_EVERY == 0:
+            times = {"A": 2, "B": 1, "C": 0}[METHOD(piece)]
+            if times >= 1:
+                half_sums = sum_pool.tile([P, PIECE_ROWS, HEAD // 2], F32)
+                nc.gpsimd.tensor_tensor(
+                    out=half_sums[:], in0=squares[:, :, 0 : HEAD // 2], in1=squares[:, :, HEAD // 2 : HEAD], op=ADD
+                )
+                partial_sums[piece] = half_sums[:]
+            if times >= 2:
                 quarter_sums = sum_pool.tile([P, PIECE_ROWS, HEAD // 4], F32)
                 nc.gpsimd.tensor_tensor(
                     out=quarter_sums[:],
@@ -193,17 +260,17 @@ def tile_lorentzmultiheadattention_pa_t_kernel(tc, x_space, Wq, bq, Wk, bk, out_
                     in1=half_sums[:, :, HEAD // 4 : HEAD // 2],
                     op=ADD,
                 )
-                partial_sums[piece] = quarter_sums
+                partial_sums[piece] = quarter_sums[:]
 
         def reduce_rows(piece):
-            norm = sum_pool.tile([P, PIECE_ROWS], F32)
-            nc.vector.tensor_reduce(out=norm[:], in_=partial_sums[piece][:], axis=mybir.AxisListType.X, op=ADD)
+            norm = sum_pool.tile([P, PIECE_HEADS, TILES], F32, name="norm")
+            nc.vector.tensor_reduce(out=norm[:].rearrange("p h t -> p (h t)"), in_=partial_sums[piece], axis=mybir.AxisListType.X, op=ADD)
             norms[piece] = norm
 
         def root_and_store(piece):
             b, c = divmod(piece, PIECES_PER_BATCH)
             rows = lifted[piece]
-            nc.scalar.activation(out=rows[:, :, 0], in_=norms[piece][:], func=SQRT, bias=one[:])
+            nc.scalar.activation(out=rows[:, :, 0], in_=norms[piece][:].rearrange("p h t -> p (h t)"), func=SQRT, bias=one[:])
             target = (out_0, out_1)[c // 2]
             first_head = PIECE_HEADS * (c % 2)
             nc.sync.dma_start(
@@ -211,21 +278,60 @@ def tile_lorentzmultiheadattention_pa_t_kernel(tc, x_space, Wq, bq, Wk, bk, out_
                 in_=rows[:].rearrange("p (h t) d -> p h (t d)", h=PIECE_HEADS),
             )
 
-        def pieces_of(r):
-            if 0 <= r < HALF_BATCHES:
-                return range(ROUND_PIECES * r, ROUND_PIECES * (r + 1))
-            return range(0)
 
-        for r in range(HALF_BATCHES + LAG_ROOT):
-            for piece in pieces_of(r - LAG_PROJECT):
-                project(piece)
-            if 0 <= r - LAG_QUANTISE < HALF_BATCHES:
-                quantise(r - LAG_QUANTISE)
-            for piece in pieces_of(r - LAG_SQUARE):
-                square(piece)
-            if r < HALF_BATCHES:
-                turn(r)
-            for piece in pieces_of(r - LAG_REDUCE):
-                reduce_rows(piece)
-            for piece in pieces_of(r - LAG_ROOT):
-                root_and_store(piece)
+        def norm_first(piece, part, parts):
+            m = METHOD(piece)
+            if m in "ABC":
+                square(piece, part, parts)
+            elif m == "E":
+                accumulate(piece, part, parts)
+
+        turn_w(0)
+        quantise_w(0)
+        turn(0, 1)
+        turn_w(1)
+        quantise(0, 1)
+        quantise_w(1)
+        turn(1, 1)
+        quantise(1, 1)
+        for c in range(2):
+            project(c, 0)
+        turn(2, 1)
+        for c in range(2, 4):
+            project(c, 0)
+        turn(3, 1)
+        quantise(2, 1)
+        quantise(3, 1)
+        for c in range(4):
+            norm_first(c, 0, 2)
+
+        for r in range(PIECES + LAG_ROOT):
+            if r < PIECES:
+                for half in range(r < 4, 2):
+                    project(r, half)
+            if r % PAIR == PAIR - 1:
+                q = r // PAIR * PAIR + UNITS_PER_BATCH
+                for k in range(PAIR // QUANT):
+                    if q + k * QUANT < UNITS:
+                        quantise(q + k * QUANT)
+            if 1 <= r < PIECES + 1 and METHOD(r - 1) == "D":
+                statistics(r - 1, 0, 1)
+            if r % PAIR == 0:
+                for k in range(PAIR):
+                    if r + UNITS_PER_BATCH + k < UNITS:
+                        turn(r + UNITS_PER_BATCH + k)
+            if r >= 1 and r - 1 < PIECES:
+                if r - 1 < 4:
+                    norm_first(r - 1, 1, 2)
+                else:
+                    norm_first(r - 1, 0, 1)
+                if METHOD(r - 1) in "ABC":
+                    halve(r - 1)
+            k = r - LAG_REDUCE
+            if 0 <= k < PIECES:
+                if METHOD(k) in "ABC":
+                    reduce_rows(k)
+                elif METHOD(k) == "D":
+                    combine(k)
+            if 0 <= r - LAG_ROOT < PIECES:
+                root_and_store(r - LAG_ROOT)

@@ -30,14 +30,21 @@ PIECE_ROWS = PIECE_HEADS * TILES
 PIECES_PER_BATCH = FEATURES // P
 PIECES = BATCHES * PIECES_PER_BATCH
 
-LAG_REDUCE = 2
+LAG_REDUCE = 3
 LAG_ROOT = 3
-QUANT = 2
-PAIR = 2
+QUANT = 4
+LEAD = 6
+QROUND = 2
+SQFIRST = 0
+TAIL = 2
+ROOTLATE = 1
+
+
+ACCUM = (1,)
 
 
 def METHOD(piece):
-    return "DEE"[piece % 3]
+    return ""[piece - PIECES + 0] if piece >= PIECES - 0 else "AAB"[piece % 3]
 
 
 FLOPS = 2 * BATCHES * TOKENS * K * FEATURES
@@ -142,7 +149,6 @@ def tile_lorentzmultiheadattention_pa_t_kernel(tc, x_space, Wq, bq, Wk, bk, out_
         scales = {}
         lifted = {}
         squares_of = {}
-        stats_of = {}
         partial_sums = {}
         norms = {}
 
@@ -200,22 +206,14 @@ def tile_lorentzmultiheadattention_pa_t_kernel(tc, x_space, Wq, bq, Wk, bk, out_
             if part == 0:
                 squares = sum_pool.tile([P, PIECE_HEADS, TILES, HEAD], F32)
                 squares_of[piece] = squares
-            ts = slice(part * TILES // parts, (part + 1) * TILES // parts)
-            nc.scalar.activation(
-                out=squares_of[piece][:, :, ts],
-                in_=lifted[piece][:, :, 1:ROW].rearrange("p (h t) d -> p h t d", h=PIECE_HEADS)[:, :, ts],
-                func=SQUARE,
-            )
-
-        def accumulate(piece, part, parts):
-            if part == 0:
-                norm = sum_pool.tile([P, PIECE_HEADS, TILES], F32, name="norm")
+                norm = sum_pool.tile([P, PIECE_HEADS, TILES], F32, name="norm", bufs=8)
                 norms[piece] = norm
-                junk = sum_pool.tile([P, PIECE_HEADS, TILES, HEAD], F32, name="squares")
-                squares_of[piece] = junk
             rows = lifted[piece][:, :, 1:ROW].rearrange("p (h t) d -> p h t d", h=PIECE_HEADS)
-            for h in range(PIECE_HEADS):
-                for t in range(part * TILES // parts, (part + 1) * TILES // parts):
+            end = (part + 1) * TILES // parts
+            ts = slice(part * TILES // parts, min(end, TILES - ACC(piece)))
+            nc.scalar.activation(out=squares_of[piece][:, :, ts], in_=rows[:, :, ts], func=SQUARE)
+            for t in range(ts.stop, end):
+                for h in range(PIECE_HEADS):
                     nc.scalar.activation(
                         out=squares_of[piece][:, h, t],
                         in_=rows[:, h, t],
@@ -223,49 +221,44 @@ def tile_lorentzmultiheadattention_pa_t_kernel(tc, x_space, Wq, bq, Wk, bk, out_
                         accum_out=norms[piece][:, h, t : t + 1],
                     )
 
-        def statistics(piece, part, parts):
-            if part == 0:
-                stats = sum_pool.tile([P, TILES, 2, 3], F32)
-                stats_of[piece] = stats
-            rows = lifted[piece][:, :, 1:ROW].rearrange("p (h t) d -> p h t d", h=PIECE_HEADS)
-            for t in range(part * TILES // parts, (part + 1) * TILES // parts):
-                nc.vector.bn_stats(
-                    out=stats_of[piece][:, t].rearrange("p h s -> p (h s)"),
-                    in_=rows[:, :, t].rearrange("p h d -> p d h"),
-                )
-
-        def combine(piece):
-            stats = stats_of[piece][:].rearrange("p t h s -> p h t s")
-            mean_part = sum_pool.tile([P, PIECE_HEADS, TILES], F32)
-            nc.scalar.activation(out=mean_part[:], in_=stats[:, :, :, 1], func=SQUARE, scale=8.0)
-            norm = sum_pool.tile([P, PIECE_HEADS, TILES], F32, name="norm")
-            nc.gpsimd.tensor_tensor(out=norm[:], in0=mean_part[:], in1=stats[:, :, :, 2], op=ADD)
-            norms[piece] = norm
+        def ACC(piece):
+            return 0 if piece >= PIECES - TAIL else ACCUM[piece % len(ACCUM)]
 
         def halve(piece):
-            squares = squares_of[piece][:].rearrange("p h t d -> p (h t) d")
+            n = TILES - ACC(piece)
+            squares = squares_of[piece][:, :, 0:n]
             partial_sums[piece] = squares
             times = {"A": 2, "B": 1, "C": 0}[METHOD(piece)]
             if times >= 1:
-                half_sums = sum_pool.tile([P, PIECE_ROWS, HEAD // 2], F32)
+                half_sums = sum_pool.tile([P, PIECE_HEADS, TILES, HEAD // 2], F32)
                 nc.gpsimd.tensor_tensor(
-                    out=half_sums[:], in0=squares[:, :, 0 : HEAD // 2], in1=squares[:, :, HEAD // 2 : HEAD], op=ADD
-                )
-                partial_sums[piece] = half_sums[:]
-            if times >= 2:
-                quarter_sums = sum_pool.tile([P, PIECE_ROWS, HEAD // 4], F32)
-                nc.gpsimd.tensor_tensor(
-                    out=quarter_sums[:],
-                    in0=half_sums[:, :, 0 : HEAD // 4],
-                    in1=half_sums[:, :, HEAD // 4 : HEAD // 2],
+                    out=half_sums[:, :, 0:n],
+                    in0=squares[:, :, :, 0 : HEAD // 2],
+                    in1=squares[:, :, :, HEAD // 2 : HEAD],
                     op=ADD,
                 )
-                partial_sums[piece] = quarter_sums[:]
+                partial_sums[piece] = half_sums[:, :, 0:n]
+            if times >= 2:
+                quarter_sums = sum_pool.tile([P, PIECE_HEADS, TILES, HEAD // 4], F32)
+                nc.gpsimd.tensor_tensor(
+                    out=quarter_sums[:, :, 0:n],
+                    in0=half_sums[:, :, 0:n, 0 : HEAD // 4],
+                    in1=half_sums[:, :, 0:n, HEAD // 4 : HEAD // 2],
+                    op=ADD,
+                )
+                partial_sums[piece] = quarter_sums[:, :, 0:n]
 
         def reduce_rows(piece):
-            norm = sum_pool.tile([P, PIECE_HEADS, TILES], F32, name="norm")
-            nc.vector.tensor_reduce(out=norm[:].rearrange("p h t -> p (h t)"), in_=partial_sums[piece], axis=mybir.AxisListType.X, op=ADD)
-            norms[piece] = norm
+            n = TILES - ACC(piece)
+            nc.vector.tensor_reduce(
+                out=norms[piece][:, :, 0:n], in_=partial_sums[piece], axis=mybir.AxisListType.X, op=ADD
+            )
+
+        def reduce_half(piece, half):
+            ts = slice(half * HALF, (half + 1) * HALF)
+            nc.vector.tensor_reduce(
+                out=norms[piece][:, :, ts], in_=squares_of[piece][:, :, ts], axis=mybir.AxisListType.X, op=ADD
+            )
 
         def root_and_store(piece):
             b, c = divmod(piece, PIECES_PER_BATCH)
@@ -279,59 +272,67 @@ def tile_lorentzmultiheadattention_pa_t_kernel(tc, x_space, Wq, bq, Wk, bk, out_
             )
 
 
-        def norm_first(piece, part, parts):
-            m = METHOD(piece)
-            if m in "ABC":
-                square(piece, part, parts)
-            elif m == "E":
-                accumulate(piece, part, parts)
-
         turn_w(0)
         quantise_w(0)
         turn(0, 1)
-        turn_w(1)
         quantise(0, 1)
-        quantise_w(1)
+        turn_w(1)
         turn(1, 1)
         quantise(1, 1)
-        for c in range(2):
-            project(c, 0)
+        quantise_w(1)
         turn(2, 1)
-        for c in range(2, 4):
-            project(c, 0)
+        project(0, 0)
+        project(1, 0)
         turn(3, 1)
+        project(2, 0)
+        project(3, 0)
         quantise(2, 1)
         quantise(3, 1)
-        for c in range(4):
-            norm_first(c, 0, 2)
+        square(0, 0, 2)
+        square(1, 0, 2)
+        turn(4)
+        square(2, 0, 2)
+        square(3, 0, 2)
+        if LEAD > 5:
+            turn(5)
+
+        def late_root(r):
+            k = r - LAG_ROOT
+            if 0 <= k < PIECES - TAIL:
+                root_and_store(k)
 
         for r in range(PIECES + LAG_ROOT):
+            if not ROOTLATE:
+                late_root(r)
+            if 4 <= r < PIECES:
+                project(r, 0)
+            if r % 4 == QROUND:
+                q = (r // 4 + 1) * 4
+                if q < UNITS:
+                    quantise(q)
             if r < PIECES:
-                for half in range(r < 4, 2):
-                    project(r, half)
-            if r % PAIR == PAIR - 1:
-                q = r // PAIR * PAIR + UNITS_PER_BATCH
-                for k in range(PAIR // QUANT):
-                    if q + k * QUANT < UNITS:
-                        quantise(q + k * QUANT)
-            if 1 <= r < PIECES + 1 and METHOD(r - 1) == "D":
-                statistics(r - 1, 0, 1)
-            if r % PAIR == 0:
-                for k in range(PAIR):
-                    if r + UNITS_PER_BATCH + k < UNITS:
-                        turn(r + UNITS_PER_BATCH + k)
-            if r >= 1 and r - 1 < PIECES:
-                if r - 1 < 4:
-                    norm_first(r - 1, 1, 2)
+                project(r, 1)
+            if SQFIRST == 0 and r + LEAD < UNITS:
+                turn(r + LEAD)
+            k = r - 1
+            if 0 <= k < PIECES - TAIL:
+                if k < 4:
+                    square(k, 1, 2)
                 else:
-                    norm_first(r - 1, 0, 1)
-                if METHOD(r - 1) in "ABC":
-                    halve(r - 1)
+                    square(k, 0, 1)
+                halve(k)
+            if SQFIRST == 1 and r + LEAD < UNITS:
+                turn(r + LEAD)
+            if PIECES - TAIL <= r < PIECES:
+                square(r, 0, 2)
+                square(r, 1, 2)
             k = r - LAG_REDUCE
-            if 0 <= k < PIECES:
-                if METHOD(k) in "ABC":
-                    reduce_rows(k)
-                elif METHOD(k) == "D":
-                    combine(k)
-            if 0 <= r - LAG_ROOT < PIECES:
-                root_and_store(r - LAG_ROOT)
+            if 0 <= k < PIECES - TAIL:
+                reduce_rows(k)
+            if ROOTLATE:
+                late_root(r)
+            k = r - 1
+            if PIECES - TAIL <= k < PIECES:
+                reduce_half(k, 0)
+                reduce_half(k, 1)
+                root_and_store(k)

@@ -26,26 +26,19 @@ UNIT = 2
 UNITS_PER_BATCH = TILES // UNIT
 UNITS = BATCHES * UNITS_PER_BATCH
 PIECE_HEADS = P // HEAD
-PIECE_ROWS = PIECE_HEADS * TILES
 PIECES_PER_BATCH = FEATURES // P
 PIECES = BATCHES * PIECES_PER_BATCH
 
-LAG_REDUCE = 3
-LAG_ROOT = 3
-QUANT = 4
 LEAD = 6
+LATE = PIECES - 6
+LAG_REDUCE = 4
+LAG_ROOT = 4
+ACC = 1
+TIMES = (2, 1)
 QROUND = 2
-SQFIRST = 0
-TAIL = 2
-ROOTLATE = 1
-
-
-ACCUM = (1,)
-
-
-def METHOD(piece):
-    return ""[piece - PIECES + 0] if piece >= PIECES - 0 else "AAB"[piece % 3]
-
+QHALF = 0
+SROOT = 1
+FILLG = 1
 
 FLOPS = 2 * BATCHES * TOKENS * K * FEATURES
 
@@ -56,15 +49,14 @@ def tile_lorentzmultiheadattention_pa_t_kernel(tc, x_space, Wq, bq, Wk, bk, out_
         stack.enter_context(tc.manual_schedule())
         const = stack.enter_context(tc.tile_pool(name="const", bufs=1))
         x_pool = stack.enter_context(tc.tile_pool(name="x", bufs=1))
-        mx_pool = stack.enter_context(tc.tile_pool(name="mx", bufs=4))
+        mx_pool = stack.enter_context(tc.tile_pool(name="mx", bufs=3))
         out_pool = stack.enter_context(tc.tile_pool(name="lifted", bufs=10))
-        sum_pool = stack.enter_context(tc.tile_pool(name="sums", bufs=4))
+        sum_pool = stack.enter_context(tc.tile_pool(name="sums", bufs=5))
         turn_banks = stack.enter_context(tc.psum_pool(name="turned", bufs=4))
         product_banks = stack.enter_context(tc.psum_pool(name="products", bufs=4))
 
-        bias_row = const.tile([1, FEATURES], BF16)
-        nc.sync.dma_start(out=bias_row[:, 0 : FEATURES // 2], in_=bq.unsqueeze(0))
-        nc.sync.dma_start(out=bias_row[:, FEATURES // 2 : FEATURES], in_=bk.unsqueeze(0))
+        bias_rows = const.tile([P, FEATURES], BF16)
+        nc.vector.memset(bias_rows[:], 0.0)
         w_raw = const.tile([P, 4 * K], BF16)
         x_words = {}
 
@@ -87,8 +79,11 @@ def tile_lorentzmultiheadattention_pa_t_kernel(tc, x_space, Wq, bq, Wk, bk, out_
 
         load_w(0, Wq)
         load_x(0, 1)
+        nc.sync.dma_start(out=bias_rows[0:1, 0 : FEATURES // 2], in_=bq.unsqueeze(0))
+        nc.sync.dma_start(out=bias_rows[0:1, FEATURES // 2 : FEATURES], in_=bk.unsqueeze(0))
+        load_x(1, 1)
         load_w(1, Wk)
-        for u in range(1, UNITS_PER_BATCH):
+        for u in range(2, UNITS_PER_BATCH):
             load_x(u, 1)
         for u in range(UNITS_PER_BATCH, UNITS, 2):
             load_x(u, 2)
@@ -99,16 +94,14 @@ def tile_lorentzmultiheadattention_pa_t_kernel(tc, x_space, Wq, bq, Wk, bk, out_
         nc.vector.memset(one[:], 1.0)
         warm = const.tile([P, 1], F32)
         nc.scalar.activation(out=warm[:], in_=one[:], func=SQRT)
-
-        bias_rows = const.tile([P, FEATURES], BF16)
-        nc.vector.memset(bias_rows[:], 0.0)
-        nc.vector.tensor_copy(out=bias_rows[0:1, :], in_=bias_row[:])
         ones = const.tile([P, P], BF16)
         nc.vector.memset(ones[:], 1.0)
-        bias_bank = product_banks.tile([P, FEATURES], F32, tag="product")
-        nc.tensor.matmul(out=bias_bank[:], lhsT=ones[:], rhs=bias_rows[:], start=True, stop=True)
         bias = const.tile([P, FEATURES], F32)
-        nc.vector.tensor_copy(out=bias[:], in_=bias_bank[:])
+
+        def spread_bias():
+            bank = product_banks.tile([P, FEATURES], F32, tag="product")
+            nc.tensor.matmul(out=bank[:], lhsT=ones[:], rhs=bias_rows[:], start=True, stop=True)
+            nc.vector.tensor_copy(out=bias[:], in_=bank[:])
 
         def turn_two_tiles(raw_words, grouped_words, copy):
             bank = turn_banks.tile([P, 4 * P], F32)
@@ -144,41 +137,43 @@ def tile_lorentzmultiheadattention_pa_t_kernel(tc, x_space, Wq, bq, Wk, bk, out_
             )
 
         grouped = {}
-        whole = {}
         codes = {}
         scales = {}
         lifted = {}
         squares_of = {}
         partial_sums = {}
         norms = {}
+        W_UNIT = 4 * UNIT * P
 
-        def turn(unit, q=QUANT):
-            if unit % q == 0:
-                x_grouped = mx_pool.tile([P, 4 * UNIT * P * q], BF16, align_bytes=64)
-            for i in range(q):
-                if unit % q == 0:
-                    grouped[unit + i] = x_grouped[:, i * 4 * UNIT * P : (i + 1) * 4 * UNIT * P]
-                    whole[unit + i] = x_grouped
-            turn_two_tiles(x_words[unit], grouped[unit].bitcast(F32), nc.scalar.copy)
+        def turn(unit):
+            b, u = divmod(unit, UNITS_PER_BATCH)
+            if u == 0:
+                x_grouped = mx_pool.tile([P, UNITS_PER_BATCH * W_UNIT], BF16, align_bytes=64)
+                grouped[b] = x_grouped
+            turn_two_tiles(x_words[unit], grouped[b][:, u * W_UNIT : (u + 1) * W_UNIT].bitcast(F32), nc.scalar.copy)
 
-        def quantise(unit, q=QUANT):
+        def quantise(unit, count):
             b, u = divmod(unit, UNITS_PER_BATCH)
             if u == 0:
                 x_codes = mx_pool.tile([P, TILES * P], U32, align_bytes=64)
                 x_scales = mx_pool.tile([P, TILES * P], U8, align_bytes=64)
                 codes[b] = x_codes
                 scales[b] = x_scales
-            cols = slice(u * UNIT * P, (u + q) * UNIT * P)
+            cols = slice(u * UNIT * P, (u + count) * UNIT * P)
             nc.vector.quantize_mx(
-                out=codes[b][:, cols].bitcast(FP8X4), scales=scales[b][:, cols], in_=whole[unit][:]
+                out=codes[b][:, cols].bitcast(FP8X4),
+                scales=scales[b][:, cols],
+                in_=grouped[b][:, u * W_UNIT : (u + count) * W_UNIT],
             )
 
         def project(piece, half):
             b, c = divmod(piece, PIECES_PER_BATCH)
             features = slice(c * P, (c + 1) * P)
             if half == 0:
-                rows = out_pool.tile([P, PIECE_ROWS, ROW], F32)
+                rows = out_pool.tile([P, PIECE_HEADS, TILES, ROW], F32)
                 lifted[piece] = rows
+                norm = sum_pool.tile([P, PIECE_HEADS, TILES], F32, bufs=8)
+                norms[piece] = norm
             product = product_banks.tile([P, HALF * P], F32)
             for i in range(HALF):
                 tokens = slice((half * HALF + i) * P, (half * HALF + i + 1) * P)
@@ -191,9 +186,8 @@ def tile_lorentzmultiheadattention_pa_t_kernel(tc, x_space, Wq, bq, Wk, bk, out_
                     start=True,
                     stop=True,
                 )
-            u_rows = lifted[piece][:, :, 1:ROW].rearrange("p (h t) d -> p h t d", h=PIECE_HEADS)
             nc.vector.tensor_tensor(
-                out=u_rows[:, :, half * HALF : (half + 1) * HALF],
+                out=lifted[piece][:, :, half * HALF : (half + 1) * HALF, 1:ROW],
                 in0=product[:].rearrange("p (t h d) -> p h t d", t=HALF, h=PIECE_HEADS),
                 in1=bias[:, features]
                 .rearrange("p (h d) -> p h d", h=PIECE_HEADS)
@@ -202,137 +196,134 @@ def tile_lorentzmultiheadattention_pa_t_kernel(tc, x_space, Wq, bq, Wk, bk, out_
                 op=ADD,
             )
 
-        def square(piece, part, parts):
-            if part == 0:
+        def square(piece, first, end):
+            if first == 0:
                 squares = sum_pool.tile([P, PIECE_HEADS, TILES, HEAD], F32)
                 squares_of[piece] = squares
-                norm = sum_pool.tile([P, PIECE_HEADS, TILES], F32, name="norm", bufs=8)
-                norms[piece] = norm
-            rows = lifted[piece][:, :, 1:ROW].rearrange("p (h t) d -> p h t d", h=PIECE_HEADS)
-            end = (part + 1) * TILES // parts
-            ts = slice(part * TILES // parts, min(end, TILES - ACC(piece)))
-            nc.scalar.activation(out=squares_of[piece][:, :, ts], in_=rows[:, :, ts], func=SQUARE)
-            for t in range(ts.stop, end):
-                for h in range(PIECE_HEADS):
+            nc.scalar.activation(
+                out=squares_of[piece][:, :, first:end], in_=lifted[piece][:, :, first:end, 1:ROW], func=SQUARE
+            )
+
+        def square_and_sum(piece, first, end):
+            for h in range(PIECE_HEADS):
+                for t in range(first, end):
                     nc.scalar.activation(
                         out=squares_of[piece][:, h, t],
-                        in_=rows[:, h, t],
+                        in_=lifted[piece][:, h, t, 1:ROW],
                         func=SQUARE,
                         accum_out=norms[piece][:, h, t : t + 1],
                     )
 
-        def ACC(piece):
-            return 0 if piece >= PIECES - TAIL else ACCUM[piece % len(ACCUM)]
-
-        def halve(piece):
-            n = TILES - ACC(piece)
-            squares = squares_of[piece][:, :, 0:n]
-            partial_sums[piece] = squares
-            times = {"A": 2, "B": 1, "C": 0}[METHOD(piece)]
-            if times >= 1:
+        def halve(piece, first, end):
+            squares = squares_of[piece]
+            if first == 0:
                 half_sums = sum_pool.tile([P, PIECE_HEADS, TILES, HEAD // 2], F32)
-                nc.gpsimd.tensor_tensor(
-                    out=half_sums[:, :, 0:n],
-                    in0=squares[:, :, :, 0 : HEAD // 2],
-                    in1=squares[:, :, :, HEAD // 2 : HEAD],
-                    op=ADD,
-                )
-                partial_sums[piece] = half_sums[:, :, 0:n]
-            if times >= 2:
-                quarter_sums = sum_pool.tile([P, PIECE_HEADS, TILES, HEAD // 4], F32)
-                nc.gpsimd.tensor_tensor(
-                    out=quarter_sums[:, :, 0:n],
-                    in0=half_sums[:, :, 0:n, 0 : HEAD // 4],
-                    in1=half_sums[:, :, 0:n, HEAD // 4 : HEAD // 2],
-                    op=ADD,
-                )
-                partial_sums[piece] = quarter_sums[:, :, 0:n]
-
-        def reduce_rows(piece):
-            n = TILES - ACC(piece)
-            nc.vector.tensor_reduce(
-                out=norms[piece][:, :, 0:n], in_=partial_sums[piece], axis=mybir.AxisListType.X, op=ADD
+                partial_sums[piece] = half_sums
+            half_sums = partial_sums[piece]
+            nc.gpsimd.tensor_tensor(
+                out=half_sums[:, :, first:end],
+                in0=squares[:, :, first:end, 0 : HEAD // 2],
+                in1=squares[:, :, first:end, HEAD // 2 : HEAD],
+                op=ADD,
             )
 
-        def reduce_half(piece, half):
-            ts = slice(half * HALF, (half + 1) * HALF)
+        def halve_again(piece, end):
+            half_sums = partial_sums[piece]
+            quarter_sums = sum_pool.tile([P, PIECE_HEADS, TILES, HEAD // 4], F32)
+            nc.gpsimd.tensor_tensor(
+                out=quarter_sums[:, :, 0:end],
+                in0=half_sums[:, :, 0:end, 0 : HEAD // 4],
+                in1=half_sums[:, :, 0:end, HEAD // 4 : HEAD // 2],
+                op=ADD,
+            )
+            partial_sums[piece] = quarter_sums
+
+        def reduce_rows(piece, source, end):
             nc.vector.tensor_reduce(
-                out=norms[piece][:, :, ts], in_=squares_of[piece][:, :, ts], axis=mybir.AxisListType.X, op=ADD
+                out=norms[piece][:, :, 0:end], in_=source[:, :, 0:end], axis=mybir.AxisListType.X, op=ADD
             )
 
         def root_and_store(piece):
             b, c = divmod(piece, PIECES_PER_BATCH)
             rows = lifted[piece]
-            nc.scalar.activation(out=rows[:, :, 0], in_=norms[piece][:].rearrange("p h t -> p (h t)"), func=SQRT, bias=one[:])
+            nc.scalar.activation(out=rows[:, :, :, 0], in_=norms[piece][:], func=SQRT, bias=one[:])
             target = (out_0, out_1)[c // 2]
             first_head = PIECE_HEADS * (c % 2)
             nc.sync.dma_start(
                 out=target[b, first_head : first_head + PIECE_HEADS].rearrange("h (p t) d -> p h (t d)", t=TILES),
-                in_=rows[:].rearrange("p (h t) d -> p h (t d)", h=PIECE_HEADS),
+                in_=rows[:].rearrange("p h t d -> p h (t d)"),
             )
 
+        SUMMED = TILES - ACC
+        BATCH0 = range(PIECES_PER_BATCH)
 
         turn_w(0)
+        turn(0)
         quantise_w(0)
-        turn(0, 1)
         quantise(0, 1)
-        turn_w(1)
-        turn(1, 1)
+        spread_bias()
+        turn(1)
         quantise(1, 1)
-        quantise_w(1)
-        turn(2, 1)
         project(0, 0)
+        turn_w(1)
         project(1, 0)
-        turn(3, 1)
+        quantise_w(1)
+        turn(2)
+        turn(3)
+        quantise(2, 1)
         project(2, 0)
         project(3, 0)
-        quantise(2, 1)
         quantise(3, 1)
-        square(0, 0, 2)
-        square(1, 0, 2)
+        for c in (0, 1):
+            square(c, 0, HALF)
+            if FILLG:
+                halve(c, 0, HALF)
         turn(4)
-        square(2, 0, 2)
-        square(3, 0, 2)
-        if LEAD > 5:
-            turn(5)
-
-        def late_root(r):
-            k = r - LAG_ROOT
-            if 0 <= k < PIECES - TAIL:
-                root_and_store(k)
+        for c in (2, 3):
+            square(c, 0, HALF)
+            if FILLG:
+                halve(c, 0, HALF)
+        turn(5)
 
         for r in range(PIECES + LAG_ROOT):
-            if not ROOTLATE:
-                late_root(r)
-            if 4 <= r < PIECES:
+            k = r - LAG_ROOT
+            if not SROOT and 0 <= k < LATE:
+                root_and_store(k)
+            if PIECES_PER_BATCH <= r < PIECES:
                 project(r, 0)
-            if r % 4 == QROUND:
-                q = (r // 4 + 1) * 4
-                if q < UNITS:
-                    quantise(q)
+            q = (r // 4 + 1) * 4
+            if r % 4 == QROUND and q < UNITS:
+                quantise(q, 2 if r < 4 or QHALF else 4)
+            if r % 4 == QROUND + 1 and q < UNITS and (r < 4 or QHALF):
+                quantise(q + 2, 2)
+            if LATE <= r - 1 < PIECES:
+                reduce_rows(r - 1, squares_of[r - 1], HALF)
             if r < PIECES:
                 project(r, 1)
-            if SQFIRST == 0 and r + LEAD < UNITS:
+            if r + LEAD < UNITS:
                 turn(r + LEAD)
             k = r - 1
-            if 0 <= k < PIECES - TAIL:
-                if k < 4:
-                    square(k, 1, 2)
+            if 0 <= k < LATE:
+                if k in BATCH0:
+                    square(k, HALF, SUMMED)
                 else:
-                    square(k, 0, 1)
-                halve(k)
-            if SQFIRST == 1 and r + LEAD < UNITS:
-                turn(r + LEAD)
-            if PIECES - TAIL <= r < PIECES:
-                square(r, 0, 2)
-                square(r, 1, 2)
+                    square(k, 0, SUMMED)
+                square_and_sum(k, SUMMED, TILES)
+                if k in BATCH0 and FILLG:
+                    halve(k, HALF, SUMMED)
+                else:
+                    halve(k, 0, SUMMED)
+                if TIMES[k % len(TIMES)] == 2:
+                    halve_again(k, SUMMED)
+            if LATE <= k < PIECES:
+                square_and_sum(k, HALF, TILES)
+            if LATE <= r < PIECES:
+                square(r, 0, HALF)
+            if LATE <= k < PIECES:
+                root_and_store(k)
             k = r - LAG_REDUCE
-            if 0 <= k < PIECES - TAIL:
-                reduce_rows(k)
-            if ROOTLATE:
-                late_root(r)
-            k = r - 1
-            if PIECES - TAIL <= k < PIECES:
-                reduce_half(k, 0)
-                reduce_half(k, 1)
+            if 0 <= k < LATE:
+                reduce_rows(k, partial_sums[k], SUMMED)
+            k = r - LAG_ROOT
+            if SROOT and 0 <= k < LATE:
                 root_and_store(k)

@@ -39,6 +39,15 @@ QROUND = 2
 QHALF = 0
 SROOT = 1
 FILLG = 1
+BIASS = 0
+W1S = 1
+DUM = 0
+HEADS = 0
+LSW = 20
+SPLIT = 0
+DUMF = 0
+DUMB = 0
+WARM = (0, 0, 0, 0, 0)
 
 FLOPS = 2 * BATCHES * TOKENS * K * FEATURES
 
@@ -52,9 +61,11 @@ def tile_lorentzmultiheadattention_pa_t_kernel(tc, x_space, Wq, bq, Wk, bk, out_
         mx_pool = stack.enter_context(tc.tile_pool(name="mx", bufs=3))
         out_pool = stack.enter_context(tc.tile_pool(name="lifted", bufs=10))
         sum_pool = stack.enter_context(tc.tile_pool(name="sums", bufs=5))
-        turn_banks = stack.enter_context(tc.psum_pool(name="turned", bufs=4))
+        turn_banks = stack.enter_context(tc.psum_pool(name="turned", bufs=3))
         product_banks = stack.enter_context(tc.psum_pool(name="products", bufs=4))
 
+        idle_banks = stack.enter_context(tc.psum_pool(name="idle", bufs=1))
+        idle_bank = idle_banks.tile([P, FEATURES], F32)
         bias_rows = const.tile([P, FEATURES], BF16)
         nc.vector.memset(bias_rows[:], 0.0)
         w_raw = const.tile([P, 4 * K], BF16)
@@ -97,11 +108,20 @@ def tile_lorentzmultiheadattention_pa_t_kernel(tc, x_space, Wq, bq, Wk, bk, out_
         ones = const.tile([P, P], BF16)
         nc.vector.memset(ones[:], 1.0)
         bias = const.tile([P, FEATURES], F32)
+        filler = const.tile([P, FEATURES], BF16)
+        nc.gpsimd.memset(filler[:], 1.0)
+
+        def keep_warm(count):
+            if count:
+                for i in range(count):
+                    nc.tensor.matmul(out=idle_bank[:], lhsT=ones[:], rhs=filler[:], start=True, stop=True)
+
+        keep_warm(WARM[0])
 
         def spread_bias():
             bank = product_banks.tile([P, FEATURES], F32, tag="product")
             nc.tensor.matmul(out=bank[:], lhsT=ones[:], rhs=bias_rows[:], start=True, stop=True)
-            nc.vector.tensor_copy(out=bias[:], in_=bank[:])
+            (nc.scalar.copy if BIASS else nc.vector.tensor_copy)(out=bias[:], in_=bank[:])
 
         def turn_two_tiles(raw_words, grouped_words, copy):
             bank = turn_banks.tile([P, 4 * P], F32)
@@ -122,11 +142,11 @@ def tile_lorentzmultiheadattention_pa_t_kernel(tc, x_space, Wq, bq, Wk, bk, out_
         w_scales = const.tile([P, FEATURES], U8, align_bytes=64)
         H = FEATURES // 2
 
-        def turn_w(j):
+        def turn_w(j, copy):
             turn_two_tiles(
                 w_raw[:].bitcast(F32)[:, 2 * j * WORDS : 2 * (j + 1) * WORDS],
                 w_grouped[:].bitcast(F32)[:, 4 * j * P : 4 * (j + 1) * P],
-                nc.vector.tensor_copy,
+                copy,
             )
 
         def quantise_w(j):
@@ -166,6 +186,18 @@ def tile_lorentzmultiheadattention_pa_t_kernel(tc, x_space, Wq, bq, Wk, bk, out_
                 in_=grouped[b][:, u * W_UNIT : (u + count) * W_UNIT],
             )
 
+        def idle_pass(n):
+            if n:
+                nc.tensor.matmul_mx(
+                    out=idle_bank[:, 0:n],
+                    lhsT=w_codes[:, 0:P].bitcast(FP8X4),
+                    lhsT_scale=w_scales[:, 0:P],
+                    rhs=w_codes[:, 0:n].bitcast(FP8X4),
+                    rhs_scale=w_scales[:, 0:n],
+                    start=True,
+                    stop=True,
+                )
+
         def project(piece, half):
             b, c = divmod(piece, PIECES_PER_BATCH)
             features = slice(c * P, (c + 1) * P)
@@ -175,6 +207,10 @@ def tile_lorentzmultiheadattention_pa_t_kernel(tc, x_space, Wq, bq, Wk, bk, out_
                 norm = sum_pool.tile([P, PIECE_HEADS, TILES], F32, bufs=8)
                 norms[piece] = norm
             product = product_banks.tile([P, HALF * P], F32)
+            if piece < 4:
+                idle_pass(DUMF)
+            elif half == 0:
+                idle_pass(DUMB if piece % 4 == 0 else DUM)
             for i in range(HALF):
                 tokens = slice((half * HALF + i) * P, (half * HALF + i + 1) * P)
                 nc.tensor.matmul_mx(
@@ -186,15 +222,23 @@ def tile_lorentzmultiheadattention_pa_t_kernel(tc, x_space, Wq, bq, Wk, bk, out_
                     start=True,
                     stop=True,
                 )
-            nc.vector.tensor_tensor(
-                out=lifted[piece][:, :, half * HALF : (half + 1) * HALF, 1:ROW],
-                in0=product[:].rearrange("p (t h d) -> p h t d", t=HALF, h=PIECE_HEADS),
-                in1=bias[:, features]
+            product_by_head = product[:].rearrange("p (t h d) -> p h t d", t=HALF, h=PIECE_HEADS)
+            bias_by_head = (
+                bias[:, features]
                 .rearrange("p (h d) -> p h d", h=PIECE_HEADS)
                 .unsqueeze(2)
-                .to_broadcast([P, PIECE_HEADS, HALF, HEAD]),
-                op=ADD,
+                .to_broadcast([P, PIECE_HEADS, HALF, HEAD])
             )
+            cuts = [(0, PIECE_HEADS)]
+            if SPLIT and piece == PIECES - 1 and half == 1:
+                cuts = [(h, h + 1) for h in range(PIECE_HEADS)]
+            for first, end in cuts:
+                nc.vector.tensor_tensor(
+                    out=lifted[piece][:, first:end, half * HALF : (half + 1) * HALF, 1:ROW],
+                    in0=product_by_head[:, first:end],
+                    in1=bias_by_head[:, first:end],
+                    op=ADD,
+                )
 
         def square(piece, first, end):
             if first == 0:
@@ -204,8 +248,8 @@ def tile_lorentzmultiheadattention_pa_t_kernel(tc, x_space, Wq, bq, Wk, bk, out_
                 out=squares_of[piece][:, :, first:end], in_=lifted[piece][:, :, first:end, 1:ROW], func=SQUARE
             )
 
-        def square_and_sum(piece, first, end):
-            for h in range(PIECE_HEADS):
+        def square_and_sum(piece, first, end, heads=range(PIECE_HEADS)):
+            for h in heads:
                 for t in range(first, end):
                     nc.scalar.activation(
                         out=squares_of[piece][:, h, t],
@@ -243,46 +287,46 @@ def tile_lorentzmultiheadattention_pa_t_kernel(tc, x_space, Wq, bq, Wk, bk, out_
                 out=norms[piece][:, :, 0:end], in_=source[:, :, 0:end], axis=mybir.AxisListType.X, op=ADD
             )
 
-        def root_and_store(piece):
+        def root_and_store(piece, first=0, end=PIECE_HEADS):
             b, c = divmod(piece, PIECES_PER_BATCH)
             rows = lifted[piece]
-            nc.scalar.activation(out=rows[:, :, :, 0], in_=norms[piece][:], func=SQRT, bias=one[:])
+            nc.scalar.activation(
+                out=rows[:, first:end, :, 0], in_=norms[piece][:, first:end], func=SQRT, bias=one[:]
+            )
             target = (out_0, out_1)[c // 2]
-            first_head = PIECE_HEADS * (c % 2)
+            head = PIECE_HEADS * (c % 2)
             nc.sync.dma_start(
-                out=target[b, first_head : first_head + PIECE_HEADS].rearrange("h (p t) d -> p h (t d)", t=TILES),
-                in_=rows[:].rearrange("p h t d -> p h (t d)"),
+                out=target[b, head + first : head + end].rearrange("h (p t) d -> p h (t d)", t=TILES),
+                in_=rows[:, first:end].rearrange("p h t d -> p h (t d)"),
             )
 
         SUMMED = TILES - ACC
         BATCH0 = range(PIECES_PER_BATCH)
 
-        turn_w(0)
+        turn_w(0, nc.vector.tensor_copy)
         turn(0)
         quantise_w(0)
-        quantise(0, 1)
         spread_bias()
+        quantise(0, 1)
         turn(1)
         quantise(1, 1)
-        project(0, 0)
-        turn_w(1)
-        project(1, 0)
+        turn_w(1, nc.scalar.copy)
         quantise_w(1)
         turn(2)
+        project(0, 0)
         turn(3)
+        project(1, 0)
         quantise(2, 1)
+        quantise(3, 1)
         project(2, 0)
         project(3, 0)
-        quantise(3, 1)
         for c in (0, 1):
             square(c, 0, HALF)
-            if FILLG:
-                halve(c, 0, HALF)
+            halve(c, 0, HALF)
         turn(4)
         for c in (2, 3):
             square(c, 0, HALF)
-            if FILLG:
-                halve(c, 0, HALF)
+            halve(c, 0, HALF)
         turn(5)
 
         for r in range(PIECES + LAG_ROOT):
@@ -315,15 +359,17 @@ def tile_lorentzmultiheadattention_pa_t_kernel(tc, x_space, Wq, bq, Wk, bk, out_
                     halve(k, 0, SUMMED)
                 if TIMES[k % len(TIMES)] == 2:
                     halve_again(k, SUMMED)
-            if LATE <= k < PIECES:
+            if LATE <= k < PIECES - HEADS:
                 square_and_sum(k, HALF, TILES)
             if LATE <= r < PIECES:
                 square(r, 0, HALF)
-            if LATE <= k < PIECES:
+            if LATE <= k < PIECES - HEADS:
                 root_and_store(k)
-            k = r - LAG_REDUCE
-            if 0 <= k < LATE:
-                reduce_rows(k, partial_sums[k], SUMMED)
-            k = r - LAG_ROOT
-            if SROOT and 0 <= k < LATE:
-                root_and_store(k)
+            elif LATE <= k < PIECES:
+                for h in range(PIECE_HEADS):
+                    square_and_sum(k, HALF, TILES, (h,))
+                    root_and_store(k, h, h + 1)
+            for k in range(LATE):
+                if k + (LAG_REDUCE if k < LSW else LAG_REDUCE - 1) == r:
+                    reduce_rows(k, partial_sums[k], SUMMED)
+                    root_and_store(k)

@@ -30,7 +30,7 @@ PIECES_PER_BATCH = FEATURES // P
 PIECES = BATCHES * PIECES_PER_BATCH
 
 LEAD = 6
-LATE = PIECES - 6
+LATE = PIECES - 7
 LAG_REDUCE = 4
 LAG_ROOT = 4
 ACC = 1
@@ -43,6 +43,9 @@ BIASS = 0
 W1S = 1
 DUM = 0
 HEADS = 0
+QPOS = 1
+QEND = 0
+TPH = 1
 LSW = 20
 SPLIT = 0
 DUMF = 0
@@ -333,17 +336,21 @@ def tile_lorentzmultiheadattention_pa_t_kernel(tc, x_space, Wq, bq, Wk, bk, out_
             k = r - LAG_ROOT
             if not SROOT and 0 <= k < LATE:
                 root_and_store(k)
+            q = (r // 4 + 1) * 4
+            if r >= 4 and r % 4 == QROUND and q < UNITS and QPOS == 0:
+                quantise(q, 4)
             if PIECES_PER_BATCH <= r < PIECES:
                 project(r, 0)
-            q = (r // 4 + 1) * 4
-            if r % 4 == QROUND and q < UNITS:
-                quantise(q, 2 if r < 4 or QHALF else 4)
-            if r % 4 == QROUND + 1 and q < UNITS and (r < 4 or QHALF):
-                quantise(q + 2, 2)
+            if r in (2, 3):
+                quantise(2 * r, 2)
+            if r >= 4 and r % 4 == QROUND and q < UNITS and QPOS == 1:
+                quantise(q, 4)
             if LATE <= r - 1 < PIECES:
                 reduce_rows(r - 1, squares_of[r - 1], HALF)
             if r < PIECES:
                 project(r, 1)
+            if r >= 4 and r % 4 == QROUND and q < UNITS and QPOS == 2:
+                quantise(q, 4)
             if r + LEAD < UNITS:
                 turn(r + LEAD)
             k = r - 1
@@ -357,7 +364,7 @@ def tile_lorentzmultiheadattention_pa_t_kernel(tc, x_space, Wq, bq, Wk, bk, out_
                     halve(k, HALF, SUMMED)
                 else:
                     halve(k, 0, SUMMED)
-                if TIMES[k % len(TIMES)] == 2:
+                if TIMES[(k + TPH) % len(TIMES)] == 2:
                     halve_again(k, SUMMED)
             if LATE <= k < PIECES - HEADS:
                 square_and_sum(k, HALF, TILES)

@@ -33,7 +33,7 @@ LEAD = 6
 LATE = PIECES - 7
 LAG_REDUCE = 4
 LAG_ROOT = 4
-ACC = 1
+ACCS = (1, 1, 1, 1)
 TIMES = (2, 1)
 QROUND = 2
 QHALF = 0
@@ -42,12 +42,12 @@ FILLG = 1
 BIASS = 0
 W1S = 1
 DUM = 0
-HEADS = 0
+HEADS = 1
 QPOS = 1
 QEND = 0
 TPH = 1
 LSW = 20
-SPLIT = 0
+SPLIT = 1
 DUMF = 0
 DUMB = 0
 WARM = (0, 0, 0, 0, 0)
@@ -303,7 +303,9 @@ def tile_lorentzmultiheadattention_pa_t_kernel(tc, x_space, Wq, bq, Wk, bk, out_
                 in_=rows[:, first:end].rearrange("p h t d -> p h (t d)"),
             )
 
-        SUMMED = TILES - ACC
+        def summed(piece):
+            return TILES - ACCS[piece % 4]
+
         BATCH0 = range(PIECES_PER_BATCH)
 
         turn_w(0, nc.vector.tensor_copy)
@@ -356,16 +358,16 @@ def tile_lorentzmultiheadattention_pa_t_kernel(tc, x_space, Wq, bq, Wk, bk, out_
             k = r - 1
             if 0 <= k < LATE:
                 if k in BATCH0:
-                    square(k, HALF, SUMMED)
+                    square(k, HALF, summed(k))
                 else:
-                    square(k, 0, SUMMED)
-                square_and_sum(k, SUMMED, TILES)
+                    square(k, 0, summed(k))
+                square_and_sum(k, summed(k), TILES)
                 if k in BATCH0 and FILLG:
-                    halve(k, HALF, SUMMED)
+                    halve(k, HALF, summed(k))
                 else:
-                    halve(k, 0, SUMMED)
+                    halve(k, 0, summed(k))
                 if TIMES[(k + TPH) % len(TIMES)] == 2:
-                    halve_again(k, SUMMED)
+                    halve_again(k, summed(k))
             if LATE <= k < PIECES - HEADS:
                 square_and_sum(k, HALF, TILES)
             if LATE <= r < PIECES:
@@ -378,5 +380,5 @@ def tile_lorentzmultiheadattention_pa_t_kernel(tc, x_space, Wq, bq, Wk, bk, out_
                     root_and_store(k, h, h + 1)
             for k in range(LATE):
                 if k + (LAG_REDUCE if k < LSW else LAG_REDUCE - 1) == r:
-                    reduce_rows(k, partial_sums[k], SUMMED)
+                    reduce_rows(k, partial_sums[k], summed(k))
                     root_and_store(k)

@@ -31,26 +31,13 @@ PIECES = BATCHES * PIECES_PER_BATCH
 
 LEAD = 6
 LATE = PIECES - 7
+LATE_REDUCED = 3
 LAG_REDUCE = 4
-LAG_ROOT = 4
-ACCS = (1, 1, 1, 1)
-TIMES = (2, 1)
-QROUND = 2
-QHALF = 0
-SROOT = 1
-FILLG = 1
-BIASS = 0
-W1S = 1
-DUM = 0
-HEADS = 1
-QPOS = 1
-QEND = 0
-TPH = 1
-LSW = 20
-SPLIT = 1
-DUMF = 0
-DUMB = 0
-WARM = (0, 0, 0, 0, 0)
+FOLD = 8
+FOLD_PASSES = 4
+FOLD_LAG = 3
+QUANTISE_ROUND = 2
+FIRST_SHORT_LAG = 18
 
 FLOPS = 2 * BATCHES * TOKENS * K * FEATURES
 
@@ -66,9 +53,7 @@ def tile_lorentzmultiheadattention_pa_t_kernel(tc, x_space, Wq, bq, Wk, bk, out_
         sum_pool = stack.enter_context(tc.tile_pool(name="sums", bufs=5))
         turn_banks = stack.enter_context(tc.psum_pool(name="turned", bufs=3))
         product_banks = stack.enter_context(tc.psum_pool(name="products", bufs=4))
-
-        idle_banks = stack.enter_context(tc.psum_pool(name="idle", bufs=1))
-        idle_bank = idle_banks.tile([P, FEATURES], F32)
+        fold_banks = stack.enter_context(tc.psum_pool(name="folded", bufs=1))
         bias_rows = const.tile([P, FEATURES], BF16)
         nc.vector.memset(bias_rows[:], 0.0)
         w_raw = const.tile([P, 4 * K], BF16)
@@ -111,20 +96,11 @@ def tile_lorentzmultiheadattention_pa_t_kernel(tc, x_space, Wq, bq, Wk, bk, out_
         ones = const.tile([P, P], BF16)
         nc.vector.memset(ones[:], 1.0)
         bias = const.tile([P, FEATURES], F32)
-        filler = const.tile([P, FEATURES], BF16)
-        nc.gpsimd.memset(filler[:], 1.0)
-
-        def keep_warm(count):
-            if count:
-                for i in range(count):
-                    nc.tensor.matmul(out=idle_bank[:], lhsT=ones[:], rhs=filler[:], start=True, stop=True)
-
-        keep_warm(WARM[0])
 
         def spread_bias():
             bank = product_banks.tile([P, FEATURES], F32, tag="product")
             nc.tensor.matmul(out=bank[:], lhsT=ones[:], rhs=bias_rows[:], start=True, stop=True)
-            (nc.scalar.copy if BIASS else nc.vector.tensor_copy)(out=bias[:], in_=bank[:])
+            nc.vector.tensor_copy(out=bias[:], in_=bank[:])
 
         def turn_two_tiles(raw_words, grouped_words, copy):
             bank = turn_banks.tile([P, 4 * P], F32)
@@ -165,6 +141,7 @@ def tile_lorentzmultiheadattention_pa_t_kernel(tc, x_space, Wq, bq, Wk, bk, out_
         lifted = {}
         squares_of = {}
         partial_sums = {}
+        folds = {}
         norms = {}
         W_UNIT = 4 * UNIT * P
 
@@ -189,18 +166,6 @@ def tile_lorentzmultiheadattention_pa_t_kernel(tc, x_space, Wq, bq, Wk, bk, out_
                 in_=grouped[b][:, u * W_UNIT : (u + count) * W_UNIT],
             )
 
-        def idle_pass(n):
-            if n:
-                nc.tensor.matmul_mx(
-                    out=idle_bank[:, 0:n],
-                    lhsT=w_codes[:, 0:P].bitcast(FP8X4),
-                    lhsT_scale=w_scales[:, 0:P],
-                    rhs=w_codes[:, 0:n].bitcast(FP8X4),
-                    rhs_scale=w_scales[:, 0:n],
-                    start=True,
-                    stop=True,
-                )
-
         def project(piece, half):
             b, c = divmod(piece, PIECES_PER_BATCH)
             features = slice(c * P, (c + 1) * P)
@@ -210,10 +175,6 @@ def tile_lorentzmultiheadattention_pa_t_kernel(tc, x_space, Wq, bq, Wk, bk, out_
                 norm = sum_pool.tile([P, PIECE_HEADS, TILES], F32, bufs=8)
                 norms[piece] = norm
             product = product_banks.tile([P, HALF * P], F32)
-            if piece < 4:
-                idle_pass(DUMF)
-            elif half == 0:
-                idle_pass(DUMB if piece % 4 == 0 else DUM)
             for i in range(HALF):
                 tokens = slice((half * HALF + i) * P, (half * HALF + i + 1) * P)
                 nc.tensor.matmul_mx(
@@ -233,7 +194,7 @@ def tile_lorentzmultiheadattention_pa_t_kernel(tc, x_space, Wq, bq, Wk, bk, out_
                 .to_broadcast([P, PIECE_HEADS, HALF, HEAD])
             )
             cuts = [(0, PIECE_HEADS)]
-            if SPLIT and piece == PIECES - 1 and half == 1:
+            if piece == PIECES - 1 and half == 1:
                 cuts = [(h, h + 1) for h in range(PIECE_HEADS)]
             for first, end in cuts:
                 nc.vector.tensor_tensor(
@@ -285,6 +246,19 @@ def tile_lorentzmultiheadattention_pa_t_kernel(tc, x_space, Wq, bq, Wk, bk, out_
             )
             partial_sums[piece] = quarter_sums
 
+        def fold(piece, first):
+            if first == 0:
+                folded = fold_banks.tile([P, PIECE_HEADS, TILES, FOLD], F32)
+                folds[piece] = folded
+            for i in range(first, first + FOLD_PASSES):
+                nc.tensor.matmul(
+                    out=folds[piece][:],
+                    lhsT=identity[:],
+                    rhs=squares_of[piece][:, :, :, i * FOLD : (i + 1) * FOLD],
+                    start=i == 0,
+                    stop=i == HEAD // FOLD - 1,
+                )
+
         def reduce_rows(piece, source, end):
             nc.vector.tensor_reduce(
                 out=norms[piece][:, :, 0:end], in_=source[:, :, 0:end], axis=mybir.AxisListType.X, op=ADD
@@ -303,10 +277,14 @@ def tile_lorentzmultiheadattention_pa_t_kernel(tc, x_space, Wq, bq, Wk, bk, out_
                 in_=rows[:, first:end].rearrange("p h t d -> p h (t d)"),
             )
 
-        def summed(piece):
-            return TILES - ACCS[piece % 4]
-
         BATCH0 = range(PIECES_PER_BATCH)
+
+        def folded_by_tensor(piece):
+            return piece not in BATCH0 and piece % PIECES_PER_BATCH == PIECES_PER_BATCH - 1
+
+        def summed(piece):
+            whole = folded_by_tensor(piece) or piece % PIECES_PER_BATCH == 0
+            return TILES if whole else TILES - 1
 
         turn_w(0, nc.vector.tensor_copy)
         turn(0)
@@ -334,51 +312,45 @@ def tile_lorentzmultiheadattention_pa_t_kernel(tc, x_space, Wq, bq, Wk, bk, out_
             halve(c, 0, HALF)
         turn(5)
 
-        for r in range(PIECES + LAG_ROOT):
-            k = r - LAG_ROOT
-            if not SROOT and 0 <= k < LATE:
-                root_and_store(k)
-            q = (r // 4 + 1) * 4
-            if r >= 4 and r % 4 == QROUND and q < UNITS and QPOS == 0:
-                quantise(q, 4)
+        for r in range(PIECES + LAG_REDUCE):
             if PIECES_PER_BATCH <= r < PIECES:
                 project(r, 0)
             if r in (2, 3):
                 quantise(2 * r, 2)
-            if r >= 4 and r % 4 == QROUND and q < UNITS and QPOS == 1:
-                quantise(q, 4)
+            next_batch = (r // PIECES_PER_BATCH + 1) * UNITS_PER_BATCH
+            if r >= PIECES_PER_BATCH and r % PIECES_PER_BATCH == QUANTISE_ROUND and next_batch < UNITS:
+                quantise(next_batch, UNITS_PER_BATCH)
             if LATE <= r - 1 < PIECES:
-                reduce_rows(r - 1, squares_of[r - 1], HALF)
+                reduce_rows(r - 1, squares_of[r - 1], LATE_REDUCED)
             if r < PIECES:
                 project(r, 1)
-            if r >= 4 and r % 4 == QROUND and q < UNITS and QPOS == 2:
-                quantise(q, 4)
             if r + LEAD < UNITS:
                 turn(r + LEAD)
+            for first in range(0, HEAD // FOLD, FOLD_PASSES):
+                k = r - FOLD_LAG - first // FOLD_PASSES
+                if 0 <= k < LATE and folded_by_tensor(k):
+                    fold(k, first)
             k = r - 1
             if 0 <= k < LATE:
-                if k in BATCH0:
-                    square(k, HALF, summed(k))
-                else:
-                    square(k, 0, summed(k))
+                start = HALF if k in BATCH0 else 0
+                square(k, start, summed(k))
                 square_and_sum(k, summed(k), TILES)
-                if k in BATCH0 and FILLG:
-                    halve(k, HALF, summed(k))
-                else:
-                    halve(k, 0, summed(k))
-                if TIMES[(k + TPH) % len(TIMES)] == 2:
-                    halve_again(k, summed(k))
-            if LATE <= k < PIECES - HEADS:
-                square_and_sum(k, HALF, TILES)
+                if not folded_by_tensor(k):
+                    halve(k, start, summed(k))
+                    if k % 2 == 0:
+                        halve_again(k, summed(k))
+            elif LATE <= k < PIECES - 1:
+                square_and_sum(k, LATE_REDUCED, TILES)
             if LATE <= r < PIECES:
-                square(r, 0, HALF)
-            if LATE <= k < PIECES - HEADS:
+                square(r, 0, LATE_REDUCED)
+            if LATE <= k < PIECES - 1:
                 root_and_store(k)
-            elif LATE <= k < PIECES:
+            elif k == PIECES - 1:
                 for h in range(PIECE_HEADS):
-                    square_and_sum(k, HALF, TILES, (h,))
+                    square_and_sum(k, LATE_REDUCED, TILES, (h,))
                     root_and_store(k, h, h + 1)
             for k in range(LATE):
-                if k + (LAG_REDUCE if k < LSW else LAG_REDUCE - 1) == r:
-                    reduce_rows(k, partial_sums[k], summed(k))
+                short = k >= FIRST_SHORT_LAG and not folded_by_tensor(k)
+                if k + (LAG_REDUCE - 1 if short else LAG_REDUCE) == r:
+                    reduce_rows(k, folds[k] if folded_by_tensor(k) else partial_sums[k], summed(k))
                     root_and_store(k)

@@ -33,6 +33,7 @@ LEAD = 6
 LATE = PIECES - 7
 LATE_REDUCED = 3
 LAG_REDUCE = 4
+WAKE_PASSES = 4
 FOLD = 8
 FOLD_PASSES = 4
 FOLD_LAG = 3
@@ -101,6 +102,17 @@ def tile_lorentzmultiheadattention_pa_t_kernel(tc, x_space, Wq, bq, Wk, bk, out_
             bank = product_banks.tile([P, FEATURES], F32, tag="product")
             nc.tensor.matmul(out=bank[:], lhsT=ones[:], rhs=bias_rows[:], start=True, stop=True)
             nc.vector.tensor_copy(out=bias[:], in_=bank[:])
+
+        def wake_tensor():
+            bank = product_banks.tile([P, FEATURES], F32, tag="product")
+            for i in range(WAKE_PASSES):
+                nc.tensor.matmul(
+                    out=bank[:].rearrange("p (c n) -> p c n", n=P),
+                    lhsT=ones[:],
+                    rhs=ones[:].unsqueeze(1).to_broadcast([P, FEATURES // P, P]),
+                    start=True,
+                    stop=True,
+                )
 
         def turn_two_tiles(raw_words, grouped_words, copy):
             bank = turn_banks.tile([P, 4 * P], F32)
@@ -286,6 +298,7 @@ def tile_lorentzmultiheadattention_pa_t_kernel(tc, x_space, Wq, bq, Wk, bk, out_
             whole = folded_by_tensor(piece) or piece % PIECES_PER_BATCH == 0
             return TILES if whole else TILES - 1
 
+        wake_tensor()
         turn_w(0, nc.vector.tensor_copy)
         turn(0)
         quantise_w(0)

@@ -55,6 +55,8 @@ def tile_lorentzmultiheadattention_pa_t_kernel(tc, x_space, Wq, bq, Wk, bk, out_
         turn_banks = stack.enter_context(tc.psum_pool(name="turned", bufs=3))
         product_banks = stack.enter_context(tc.psum_pool(name="products", bufs=4))
         fold_banks = stack.enter_context(tc.psum_pool(name="folded", bufs=1))
+        ones = const.tile([P, P], BF16)
+        nc.vector.memset(ones[:], 1.0)
         bias_rows = const.tile([P, FEATURES], BF16)
         nc.vector.memset(bias_rows[:], 0.0)
         w_raw = const.tile([P, 4 * K], BF16)
@@ -77,7 +79,8 @@ def tile_lorentzmultiheadattention_pa_t_kernel(tc, x_space, Wq, bq, Wk, bk, out_
             for i in range(count):
                 x_words[first_unit + i] = words[:, i * UNIT * WORDS : (i + 1) * UNIT * WORDS]
 
-        load_w(0, Wq)
+        for c in range(2):
+            nc.sync.dma_start(out=w_raw[:, c * K : (c + 1) * K], in_=Wq[c * P : (c + 1) * P, :])
         load_x(0, 1)
         nc.sync.dma_start(out=bias_rows[0:1, 0 : FEATURES // 2], in_=bq.unsqueeze(0))
         nc.sync.dma_start(out=bias_rows[0:1, FEATURES // 2 : FEATURES], in_=bk.unsqueeze(0))
@@ -94,8 +97,6 @@ def tile_lorentzmultiheadattention_pa_t_kernel(tc, x_space, Wq, bq, Wk, bk, out_
         nc.vector.memset(one[:], 1.0)
         warm = const.tile([P, 1], F32)
         nc.scalar.activation(out=warm[:], in_=one[:], func=SQRT)
-        ones = const.tile([P, P], BF16)
-        nc.vector.memset(ones[:], 1.0)
         bias = const.tile([P, FEATURES], F32)
 
         def spread_bias():
@@ -103,11 +104,12 @@ def tile_lorentzmultiheadattention_pa_t_kernel(tc, x_space, Wq, bq, Wk, bk, out_
             nc.tensor.matmul(out=bank[:], lhsT=ones[:], rhs=bias_rows[:], start=True, stop=True)
             nc.vector.tensor_copy(out=bias[:], in_=bank[:])
 
-        def wake_tensor():
-            bank = product_banks.tile([P, FEATURES], F32, tag="product")
-            for i in range(WAKE_PASSES):
+        idle_bank = fold_banks.tile([P, FEATURES], F32, tag="folded")
+
+        def keep_awake(passes):
+            for i in range(passes):
                 nc.tensor.matmul(
-                    out=bank[:].rearrange("p (c n) -> p c n", n=P),
+                    out=idle_bank[:].rearrange("p (c n) -> p c n", n=P),
                     lhsT=ones[:],
                     rhs=ones[:].unsqueeze(1).to_broadcast([P, FEATURES // P, P]),
                     start=True,
@@ -298,17 +300,20 @@ def tile_lorentzmultiheadattention_pa_t_kernel(tc, x_space, Wq, bq, Wk, bk, out_
             whole = folded_by_tensor(piece) or piece % PIECES_PER_BATCH == 0
             return TILES if whole else TILES - 1
 
-        wake_tensor()
+        keep_awake(WAKE_PASSES)
         turn_w(0, nc.vector.tensor_copy)
         turn(0)
         quantise_w(0)
         spread_bias()
+        keep_awake(1)
         quantise(0, 1)
         turn(1)
         quantise(1, 1)
         turn_w(1, nc.scalar.copy)
         quantise_w(1)
+        keep_awake(1)
         turn(2)
+        keep_awake(1)
         project(0, 0)
         turn(3)
         project(1, 0)
@@ -337,6 +342,8 @@ def tile_lorentzmultiheadattention_pa_t_kernel(tc, x_space, Wq, bq, Wk, bk, out_
                 reduce_rows(r - 1, squares_of[r - 1], LATE_REDUCED)
             if r < PIECES:
                 project(r, 1)
+            if r in BATCH0:
+                keep_awake(1)
             if r + LEAD < UNITS:
                 turn(r + LEAD)
             for first in range(0, HEAD // FOLD, FOLD_PASSES):

@@ -106,12 +106,12 @@ def tile_lorentzmultiheadattention_pa_t_kernel(tc, x_space, Wq, bq, Wk, bk, out_
 
         idle_bank = fold_banks.tile([P, FEATURES], F32, tag="folded")
 
-        def keep_awake(passes):
+        def keep_awake(passes, columns=FEATURES):
             for i in range(passes):
                 nc.tensor.matmul(
-                    out=idle_bank[:].rearrange("p (c n) -> p c n", n=P),
+                    out=idle_bank[:, 0:columns].rearrange("p (c n) -> p c n", n=P),
                     lhsT=ones[:],
-                    rhs=ones[:].unsqueeze(1).to_broadcast([P, FEATURES // P, P]),
+                    rhs=ones[:].unsqueeze(1).to_broadcast([P, columns // P, P]),
                     start=True,
                     stop=True,
                 )
@@ -343,7 +343,7 @@ def tile_lorentzmultiheadattention_pa_t_kernel(tc, x_space, Wq, bq, Wk, bk, out_
             if r < PIECES:
                 project(r, 1)
             if r in BATCH0:
-                keep_awake(1)
+                keep_awake(1, FEATURES // 2)
             if r + LEAD < UNITS:
                 turn(r + LEAD)
             for first in range(0, HEAD // FOLD, FOLD_PASSES):

from contextlib import ExitStack

import concourse.mybir as mybir
from concourse.masks import make_identity

F32 = mybir.dt.float32
BF16 = mybir.dt.bfloat16
U32 = mybir.dt.uint32
U8 = mybir.dt.uint8
FP8X4 = mybir.dt.float8_e4m3fn_x4
ADD = mybir.AluOpType.add
SQUARE = mybir.ActivationFunctionType.Square
SQRT = mybir.ActivationFunctionType.Sqrt

P = 128
BATCHES = 8
TOKENS = 1024
K = 512
WORDS = K // 2
FEATURES = 512
HEAD = 64
ROW = HEAD + 1
TILES = TOKENS // P
HALF = TILES // 2
UNIT = 2
UNITS_PER_BATCH = TILES // UNIT
UNITS = BATCHES * UNITS_PER_BATCH
PIECE_HEADS = P // HEAD
PIECES_PER_BATCH = FEATURES // P
PIECES = BATCHES * PIECES_PER_BATCH

LEAD = 6
LATE = PIECES - 7
LATE_REDUCED = 3
LAG_REDUCE = 4
WAKE_PASSES = 4
FOLD = 8
FOLD_PASSES = 4
FOLD_LAG = 3
QUANTISE_ROUND = 2
FIRST_SHORT_LAG = 18

FLOPS = 2 * BATCHES * TOKENS * K * FEATURES


def tile_lorentzmultiheadattention_pa_t_kernel(tc, x_space, Wq, bq, Wk, bk, out_0, out_1):
    nc = tc.nc
    with ExitStack() as stack:
        stack.enter_context(tc.manual_schedule())
        const = stack.enter_context(tc.tile_pool(name="const", bufs=1))
        x_pool = stack.enter_context(tc.tile_pool(name="x", bufs=1))
        mx_pool = stack.enter_context(tc.tile_pool(name="mx", bufs=3))
        out_pool = stack.enter_context(tc.tile_pool(name="lifted", bufs=10))
        sum_pool = stack.enter_context(tc.tile_pool(name="sums", bufs=5))
        turn_banks = stack.enter_context(tc.psum_pool(name="turned", bufs=3))
        product_banks = stack.enter_context(tc.psum_pool(name="products", bufs=4))
        fold_banks = stack.enter_context(tc.psum_pool(name="folded", bufs=1))
        ones = const.tile([P, P], BF16)
        nc.vector.memset(ones[:], 1.0)
        bias_rows = const.tile([P, FEATURES], BF16)
        nc.vector.memset(bias_rows[:], 0.0)
        w_raw = const.tile([P, 4 * K], BF16)
        x_words = {}

        def load_w(half, W):
            nc.sync.dma_start(
                out=w_raw[:, half * 2 * K : (half + 1) * 2 * K].rearrange("p (c k) -> p c k", c=2),
                in_=W.rearrange("(c p) k -> p c k", p=P),
            )

        def load_x(first_unit, count):
            b, u = divmod(first_unit, UNITS_PER_BATCH)
            x_raw = x_pool.tile([P, count * UNIT, K], BF16, name="x%d" % first_unit)
            nc.sync.dma_start(
                out=x_raw[:],
                in_=x_space[b].rearrange("(p t) k -> p t k", t=TILES)[:, u * UNIT : (u + count) * UNIT, :],
            )
            words = x_raw[:].rearrange("p t k -> p (t k)").bitcast(F32)
            for i in range(count):
                x_words[first_unit + i] = words[:, i * UNIT * WORDS : (i + 1) * UNIT * WORDS]

        for c in range(2):
            nc.sync.dma_start(out=w_raw[:, c * K : (c + 1) * K], in_=Wq[c * P : (c + 1) * P, :])
        load_x(0, 1)
        nc.sync.dma_start(out=bias_rows[0:1, 0 : FEATURES // 2], in_=bq.unsqueeze(0))
        nc.sync.dma_start(out=bias_rows[0:1, FEATURES // 2 : FEATURES], in_=bk.unsqueeze(0))
        load_x(1, 1)
        load_w(1, Wk)
        for u in range(2, UNITS_PER_BATCH):
            load_x(u, 1)
        for u in range(UNITS_PER_BATCH, UNITS, 2):
            load_x(u, 2)

        identity = const.tile([P, P], F32)
        make_identity(nc, identity[:])
        one = const.tile([P, 1], F32)
        nc.vector.memset(one[:], 1.0)
        warm = const.tile([P, 1], F32)
        nc.scalar.activation(out=warm[:], in_=one[:], func=SQRT)
        bias = const.tile([P, FEATURES], F32)

        def spread_bias():
            bank = product_banks.tile([P, FEATURES], F32, tag="product")
            nc.tensor.matmul(out=bank[:], lhsT=ones[:], rhs=bias_rows[:], start=True, stop=True)
            nc.vector.tensor_copy(out=bias[:], in_=bank[:])

        idle_bank = fold_banks.tile([P, FEATURES], F32, tag="folded")

        def keep_awake(passes, columns=FEATURES):
            for i in range(passes):
                nc.tensor.matmul(
                    out=idle_bank[:, 0:columns].rearrange("p (c n) -> p c n", n=P),
                    lhsT=ones[:],
                    rhs=ones[:].unsqueeze(1).to_broadcast([P, columns // P, P]),
                    start=True,
                    stop=True,
                )

        def turn_two_tiles(raw_words, grouped_words, copy):
            bank = turn_banks.tile([P, 4 * P], F32)
            for i in range(2):
                for u in range(2):
                    nc.tensor.transpose(
                        bank[:, (2 * i + u) * P : (2 * i + u + 1) * P],
                        raw_words[:, i * WORDS + u : (i + 1) * WORDS : 2],
                        identity[:],
                    )
            copy(
                out=grouped_words.rearrange("p (i r u) -> p i r u", i=2, u=2),
                in_=bank[:].rearrange("p (i u r) -> p i r u", i=2, u=2),
            )

        w_grouped = const.tile([P, 4 * FEATURES], BF16, align_bytes=64)
        w_codes = const.tile([P, FEATURES], U32, align_bytes=64)
        w_scales = const.tile([P, FEATURES], U8, align_bytes=64)
        H = FEATURES // 2

        def turn_w(j, copy):
            turn_two_tiles(
                w_raw[:].bitcast(F32)[:, 2 * j * WORDS : 2 * (j + 1) * WORDS],
                w_grouped[:].bitcast(F32)[:, 4 * j * P : 4 * (j + 1) * P],
                copy,
            )

        def quantise_w(j):
            nc.vector.quantize_mx(
                out=w_codes[:, j * H : (j + 1) * H].bitcast(FP8X4),
                scales=w_scales[:, j * H : (j + 1) * H],
                in_=w_grouped[:, 4 * j * H : 4 * (j + 1) * H],
            )

        grouped = {}
        codes = {}
        scales = {}
        lifted = {}
        squares_of = {}
        partial_sums = {}
        folds = {}
        norms = {}
        W_UNIT = 4 * UNIT * P

        def turn(unit):
            b, u = divmod(unit, UNITS_PER_BATCH)
            if u == 0:
                x_grouped = mx_pool.tile([P, UNITS_PER_BATCH * W_UNIT], BF16, align_bytes=64)
                grouped[b] = x_grouped
            turn_two_tiles(x_words[unit], grouped[b][:, u * W_UNIT : (u + 1) * W_UNIT].bitcast(F32), nc.scalar.copy)

        def quantise(unit, count):
            b, u = divmod(unit, UNITS_PER_BATCH)
            if u == 0:
                x_codes = mx_pool.tile([P, TILES * P], U32, align_bytes=64)
                x_scales = mx_pool.tile([P, TILES * P], U8, align_bytes=64)
                codes[b] = x_codes
                scales[b] = x_scales
            cols = slice(u * UNIT * P, (u + count) * UNIT * P)
            nc.vector.quantize_mx(
                out=codes[b][:, cols].bitcast(FP8X4),
                scales=scales[b][:, cols],
                in_=grouped[b][:, u * W_UNIT : (u + count) * W_UNIT],
            )

        def project(piece, half):
            b, c = divmod(piece, PIECES_PER_BATCH)
            features = slice(c * P, (c + 1) * P)
            if half == 0:
                rows = out_pool.tile([P, PIECE_HEADS, TILES, ROW], F32)
                lifted[piece] = rows
                norm = sum_pool.tile([P, PIECE_HEADS, TILES], F32, bufs=8)
                norms[piece] = norm
            product = product_banks.tile([P, HALF * P], F32)
            for i in range(HALF):
                tokens = slice((half * HALF + i) * P, (half * HALF + i + 1) * P)
                nc.tensor.matmul_mx(
                    out=product[:, i * P : (i + 1) * P],
                    lhsT=codes[b][:, tokens].bitcast(FP8X4),
                    lhsT_scale=scales[b][:, tokens],
                    rhs=w_codes[:, features].bitcast(FP8X4),
                    rhs_scale=w_scales[:, features],
                    start=True,
                    stop=True,
                )
            product_by_head = product[:].rearrange("p (t h d) -> p h t d", t=HALF, h=PIECE_HEADS)
            bias_by_head = (
                bias[:, features]
                .rearrange("p (h d) -> p h d", h=PIECE_HEADS)
                .unsqueeze(2)
                .to_broadcast([P, PIECE_HEADS, HALF, HEAD])
            )
            cuts = [(0, PIECE_HEADS)]
            if piece == PIECES - 1 and half == 1:
                cuts = [(h, h + 1) for h in range(PIECE_HEADS)]
            for first, end in cuts:
                nc.vector.tensor_tensor(
                    out=lifted[piece][:, first:end, half * HALF : (half + 1) * HALF, 1:ROW],
                    in0=product_by_head[:, first:end],
                    in1=bias_by_head[:, first:end],
                    op=ADD,
                )

        def square(piece, first, end):
            if first == 0:
                squares = sum_pool.tile([P, PIECE_HEADS, TILES, HEAD], F32)
                squares_of[piece] = squares
            nc.scalar.activation(
                out=squares_of[piece][:, :, first:end], in_=lifted[piece][:, :, first:end, 1:ROW], func=SQUARE
            )

        def square_and_sum(piece, first, end, heads=range(PIECE_HEADS)):
            for h in heads:
                for t in range(first, end):
                    nc.scalar.activation(
                        out=squares_of[piece][:, h, t],
                        in_=lifted[piece][:, h, t, 1:ROW],
                        func=SQUARE,
                        accum_out=norms[piece][:, h, t : t + 1],
                    )

        def halve(piece, first, end):
            squares = squares_of[piece]
            if first == 0:
                half_sums = sum_pool.tile([P, PIECE_HEADS, TILES, HEAD // 2], F32)
                partial_sums[piece] = half_sums
            half_sums = partial_sums[piece]
            nc.gpsimd.tensor_tensor(
                out=half_sums[:, :, first:end],
                in0=squares[:, :, first:end, 0 : HEAD // 2],
                in1=squares[:, :, first:end, HEAD // 2 : HEAD],
                op=ADD,
            )

        def halve_again(piece, end):
            half_sums = partial_sums[piece]
            quarter_sums = sum_pool.tile([P, PIECE_HEADS, TILES, HEAD // 4], F32)
            nc.gpsimd.tensor_tensor(
                out=quarter_sums[:, :, 0:end],
                in0=half_sums[:, :, 0:end, 0 : HEAD // 4],
                in1=half_sums[:, :, 0:end, HEAD // 4 : HEAD // 2],
                op=ADD,
            )
            partial_sums[piece] = quarter_sums

        def fold(piece, first):
            if first == 0:
                folded = fold_banks.tile([P, PIECE_HEADS, TILES, FOLD], F32)
                folds[piece] = folded
            for i in range(first, first + FOLD_PASSES):
                nc.tensor.matmul(
                    out=folds[piece][:],
                    lhsT=identity[:],
                    rhs=squares_of[piece][:, :, :, i * FOLD : (i + 1) * FOLD],
                    start=i == 0,
                    stop=i == HEAD // FOLD - 1,
                )

        def reduce_rows(piece, source, end):
            nc.vector.tensor_reduce(
                out=norms[piece][:, :, 0:end], in_=source[:, :, 0:end], axis=mybir.AxisListType.X, op=ADD
            )

        def root_and_store(piece, first=0, end=PIECE_HEADS):
            b, c = divmod(piece, PIECES_PER_BATCH)
            rows = lifted[piece]
            nc.scalar.activation(
                out=rows[:, first:end, :, 0], in_=norms[piece][:, first:end], func=SQRT, bias=one[:]
            )
            target = (out_0, out_1)[c // 2]
            head = PIECE_HEADS * (c % 2)
            nc.sync.dma_start(
                out=target[b, head + first : head + end].rearrange("h (p t) d -> p h (t d)", t=TILES),
                in_=rows[:, first:end].rearrange("p h t d -> p h (t d)"),
            )

        BATCH0 = range(PIECES_PER_BATCH)

        def folded_by_tensor(piece):
            return piece not in BATCH0 and piece % PIECES_PER_BATCH == PIECES_PER_BATCH - 1

        def summed(piece):
            whole = folded_by_tensor(piece) or piece % PIECES_PER_BATCH == 0
            return TILES if whole else TILES - 1

        keep_awake(WAKE_PASSES)
        turn_w(0, nc.vector.tensor_copy)
        turn(0)
        quantise_w(0)
        spread_bias()
        keep_awake(1)
        quantise(0, 1)
        turn(1)
        quantise(1, 1)
        turn_w(1, nc.scalar.copy)
        quantise_w(1)
        keep_awake(1)
        turn(2)
        keep_awake(1)
        project(0, 0)
        turn(3)
        project(1, 0)
        quantise(2, 1)
        quantise(3, 1)
        project(2, 0)
        project(3, 0)
        for c in (0, 1):
            square(c, 0, HALF)
            halve(c, 0, HALF)
        turn(4)
        for c in (2, 3):
            square(c, 0, HALF)
            halve(c, 0, HALF)
        turn(5)

        for r in range(PIECES + LAG_REDUCE):
            if PIECES_PER_BATCH <= r < PIECES:
                project(r, 0)
            if r in (2, 3):
                quantise(2 * r, 2)
            next_batch = (r // PIECES_PER_BATCH + 1) * UNITS_PER_BATCH
            if r >= PIECES_PER_BATCH and r % PIECES_PER_BATCH == QUANTISE_ROUND and next_batch < UNITS:
                quantise(next_batch, UNITS_PER_BATCH)
            if LATE <= r - 1 < PIECES:
                reduce_rows(r - 1, squares_of[r - 1], LATE_REDUCED)
            if r < PIECES:
                project(r, 1)
            if r in BATCH0:
                keep_awake(1, FEATURES // 2)
            if r + LEAD < UNITS:
                turn(r + LEAD)
            for first in range(0, HEAD // FOLD, FOLD_PASSES):
                k = r - FOLD_LAG - first // FOLD_PASSES
                if 0 <= k < LATE and folded_by_tensor(k):
                    fold(k, first)
            k = r - 1
            if 0 <= k < LATE:
                start = HALF if k in BATCH0 else 0
                square(k, start, summed(k))
                square_and_sum(k, summed(k), TILES)
                if not folded_by_tensor(k):
                    halve(k, start, summed(k))
                    if k % 2 == 0:
                        halve_again(k, summed(k))
            elif LATE <= k < PIECES - 1:
                square_and_sum(k, LATE_REDUCED, TILES)
            if LATE <= r < PIECES:
                square(r, 0, LATE_REDUCED)
            if LATE <= k < PIECES - 1:
                root_and_store(k)
            elif k == PIECES - 1:
                for h in range(PIECE_HEADS):
                    square_and_sum(k, LATE_REDUCED, TILES, (h,))
                    root_and_store(k, h, h + 1)
            for k in range(LATE):
                short = k >= FIRST_SHORT_LAG and not folded_by_tensor(k)
                if k + (LAG_REDUCE - 1 if short else LAG_REDUCE) == r:
                    reduce_rows(k, folds[k] if folded_by_tensor(k) else partial_sums[k], summed(k))
                    root_and_store(k)
